import numpy as np
import ml_dtypes


def mxq(x, axis, fmt="e4m3"):
    dtype, down = {"e4m3": (ml_dtypes.float8_e4m3fn, 7), "e5m2": (ml_dtypes.float8_e5m2, 14)}[fmt]
    v = np.moveaxis(np.asarray(x, np.float32).astype(ml_dtypes.bfloat16).astype(np.float64), axis, -1)
    blocks = v.reshape(v.shape[:-1] + (-1, 32))
    amax = np.abs(blocks).max(-1, keepdims=True)
    byte = np.maximum(np.where(amax > 0, np.frexp(amax)[1] - 1 + 127, 0) - down, 1)
    scale = np.exp2(byte - 127.0)
    codes = (blocks / scale).astype(np.float32).astype(dtype).astype(np.float64)
    return np.moveaxis((codes * scale).reshape(v.shape), -1, axis)


WIDE = False


def mx_kscale(k):
    if not WIDE:
        return np.ones(k)
    levels = np.array([10, -10, 5, -5, 0])
    if k % 512:
        return np.exp2(np.random.permutation(np.resize(levels, k // 32))).repeat(32)
    a = np.empty((k // 512, 16))
    for p in range(k // 512):
        a[p, :8] = np.random.permutation(np.resize(levels, 8))
        for g in range(8):
            far = levels[np.abs(levels - a[p, g]) >= 10]
            a[p, g + 8] = far[np.random.randint(len(far))]
    return np.exp2(a.ravel()).repeat(32)


BF16 = ml_dtypes.bfloat16


def bf(x):
    return np.asarray(x, np.float32).astype(BF16)


def f64(x):
    return np.asarray(x).astype(np.float64)


B, S, HID, NH, HD, RD, RATIO = 1, 2048, 1024, 8, 128, 64, 4
THETA = 10000.0
NW = S // RATIO
HALF = RD // 2


def rope_tables(positions):
    inv_freq = 1.0 / THETA ** (np.arange(HALF) / HALF)
    ang = positions[:, None] * inv_freq[None, :]
    return np.cos(ang), np.sin(ang)


def rope_interleaved(x, cos, sin):
    nope, rope = x[..., :-RD], x[..., -RD:]
    pr = rope.reshape(rope.shape[:-1] + (HALF, 2))
    a, b = pr[..., 0], pr[..., 1]
    new = np.stack([a * cos - b * sin, a * sin + b * cos], axis=-1).reshape(rope.shape)
    return np.concatenate([nope, new], axis=-1)


def remap(t, fill):
    cur = t[..., HD:]
    prev = np.concatenate([np.full((B, 1, RATIO, HD), fill), t[:, :-1, :, :HD]], axis=1)
    return np.concatenate([prev, cur], axis=2)


def pool_overlap(kv, gate, ape):
    kv_o = remap(kv.reshape(B, NW, RATIO, 2 * HD), 0.0)
    gate_o = remap(gate.reshape(B, NW, RATIO, 2 * HD) + ape, -np.inf)
    e = np.exp(gate_o - gate_o.max(axis=2, keepdims=True))
    w = e / e.sum(axis=2, keepdims=True)
    return (kv_o * w).sum(axis=2)


def draw0():
    s = mx_kscale(HID)
    return {"hidden": bf(np.random.standard_normal((B, S, HID)) * s),
            "wkv": bf(np.random.standard_normal((HID, 2 * HD)) * 2.0 / np.sqrt(HID) / s[:, None]),
            "wgate": bf(np.random.standard_normal((HID, 2 * HD)) / np.sqrt(HID) / s[:, None]),
            "ape": bf(np.random.standard_normal((RATIO, 2 * HD)) * 0.5)}


def core(hidden, wkv, wgate, ape):
    hq = mxq(f64(hidden), 2, "e4m3")
    kv = hq @ mxq(f64(wkv), 0, "e4m3")
    gate = hq @ mxq(f64(wgate), 0, "e4m3")
    pooled = pool_overlap(kv, gate, f64(ape))
    ck, sk = rope_tables(np.arange(NW) * RATIO)
    k_rot = rope_interleaved(pooled, ck, sk)
    return k_rot, pooled


def e4m3fn_bytes(y):
    return np.clip(np.asarray(y, np.float64), -448.0, 448.0).astype(np.float32).astype(ml_dtypes.float8_e4m3fn).view(np.uint8)


def e4m3fn_values(b):
    return np.asarray(b, np.uint8).view(ml_dtypes.float8_e4m3fn).astype(np.float64)


def setup_inputs():
    d = draw0()
    x0 = np.asarray(d['hidden']).astype(np.float64)
    s = (np.max(np.abs(x0), axis=(0, 1), keepdims=True) / 448.0).astype(np.float32)
    out = {}
    for k, v in d.items():
        if k == 'hidden':
            out['hidden_bytes'] = e4m3fn_bytes(x0 / s.astype(np.float64))
            out['hidden_scale'] = s
        else:
            out[k] = v
    return out


def reference(hidden_bytes, hidden_scale, wkv, wgate, ape):
    return core(e4m3fn_values(hidden_bytes) * hidden_scale.astype(np.float64), wkv, wgate, ape)

@@ -1,0 +1,332 @@
+import math
+from contextlib import ExitStack
+
+import concourse.mybir as mybir
+from concourse.masks import make_identity
+
+FLOPS = 2 * 2048 * 1024 * 512
+
+F32 = mybir.dt.float32
+BF16 = mybir.dt.bfloat16
+I32 = mybir.dt.int32
+U32 = mybir.dt.uint32
+U8 = mybir.dt.uint8
+FP8 = mybir.dt.float8_e4m3fn
+FP8X4 = mybir.dt.float8_e4m3fn_x4
+ALU = mybir.AluOpType
+ACT = mybir.ActivationFunctionType
+
+P = 128
+HID = 1024
+NW = 512
+RATIO = 4
+NCH = 4
+HALF = 32
+THETA = 10000.0
+GW = 520
+TWO_PI = 2.0 * math.pi
+PARTS = (1, 1, 1, 2)
+GATE = 0
+KV = 1
+
+
+def tile_deepseekv4attention_pa_kernel(tc, hidden_bytes, hidden_scale, wkv, wgate, ape, out_0, out_1):
+    nc = tc.nc
+    hb_view = hidden_bytes.rearrange("o (c w r) k -> o r c w k", c=NCH, w=P, r=RATIO)[0]
+    o0_view = out_0.rearrange("o (c p) f -> o c p f", p=P)[0]
+    o1_view = out_1.rearrange("o (c p) f -> o c p f", p=P)[0]
+
+    with ExitStack() as ctx:
+        const = ctx.enter_context(tc.tile_pool(name="const", bufs=1))
+        bytes_pool = ctx.enter_context(tc.tile_pool(name="bytes", bufs=1))
+        xb_pool = ctx.enter_context(tc.tile_pool(name="xb", bufs=6))
+        grp_pool = ctx.enter_context(tc.tile_pool(name="grp", bufs=2))
+        code_pool = ctx.enter_context(tc.tile_pool(name="codes", bufs=2))
+        fin_pool = ctx.enter_context(tc.tile_pool(name="fin", bufs=4))
+        ps_xt = ctx.enter_context(tc.psum_pool(name="ps_xt", bufs=4))
+        ps_mx = ctx.enter_context(tc.psum_pool(name="ps_mx", bufs=1))
+        ctx.enter_context(tc.manual_schedule())
+
+        scale_bc = const.tile([P, HID], F32, name="scale_bc")
+        nc.scalar.dma_start(out=scale_bc, in_=hidden_scale.rearrange("a b k -> (a b k)").partition_broadcast(P))
+        hb = {}
+
+        def load_bytes(i):
+            t = bytes_pool.tile([P, HID], U8, name="hb_%d" % i)
+            nc.sync.dma_start(out=t, in_=hb_view[i // NCH, i % NCH])
+            hb[i] = t
+
+        wraw = {}
+
+        def load_w(key, w):
+            t = const.tile([P, 2, 4, 256], BF16, name="wraw_" + key)
+            nc.sync.dma_start(out=t, in_=w.rearrange("(g p j) n -> p g j n", g=2, p=P, j=4))
+            wraw[key] = t
+
+        load_bytes(0)
+        load_bytes(1)
+        load_bytes(2)
+        load_w("gate", wgate)
+        load_w("kv", wkv)
+        for i in range(3, RATIO * NCH):
+            load_bytes(i)
+
+        ape_b = []
+        with nc.allow_non_contiguous_dma(reason="ape: 1024 values, one feature to a partition"):
+            for h in range(2):
+                t = const.tile([P, RATIO], BF16, name="ape_b%d" % h)
+                nc.scalar.dma_start(out=t, in_=ape[:, h * P:(h + 1) * P].rearrange("r f -> f r"))
+                ape_b.append(t)
+
+        pos_i = const.tile([P, NCH], I32, name="pos_i")
+        nc.gpsimd.iota(pos_i, pattern=[[RATIO * P, NCH]], base=0, channel_multiplier=RATIO)
+        ident = const.tile([P, P], F32, name="ident")
+        make_identity(nc, ident)
+        g8 = const.tile([P, 8, GW], F32, name="g8")
+        kv8 = const.tile([P, 8, GW], F32, name="kv8")
+        nc.gpsimd.memset(g8[:, 0:4, 0:1], -1.0e30)
+        nc.gpsimd.memset(kv8[:, 0:4, 0:1], 0.0)
+        ape_t = const.tile([P, 8], F32, name="ape_t")
+        for h in range(2):
+            nc.gpsimd.tensor_copy(out=ape_t[:, 4 * h:4 * h + 4], in_=ape_b[h])
+
+        pos = const.tile([P, NCH], F32, name="pos")
+        nc.vector.tensor_copy(out=pos, in_=pos_i)
+        coarse = const.tile([P, NCH, 4], F32, name="coarse")
+        for a in range(4):
+            nc.vector.tensor_scalar(out=coarse[:, :, a], in0=pos, scalar1=THETA ** (-8 * a / HALF), scalar2=None, op0=ALU.mult)
+        turns = const.tile([P, NCH * 4, 8], F32, name="turns")
+        for b in range(8):
+            nc.vector.tensor_scalar(out=turns[:, :, b], in0=coarse.rearrange("p c a -> p (c a)"), scalar1=THETA ** (-b / HALF) / TWO_PI, scalar2=None, op0=ALU.mult)
+        turns_f = turns.rearrange("p q b -> p (q b)")
+        whole_i = const.tile([P, NCH * HALF], I32, name="whole_i")
+        nc.vector.tensor_copy(out=whole_i, in_=turns_f)
+        whole = const.tile([P, NCH * HALF], F32, name="whole")
+        nc.vector.tensor_copy(out=whole, in_=whole_i)
+        frac = const.tile([P, NCH * HALF], F32, name="frac")
+        nc.vector.tensor_tensor(out=frac, in0=turns_f, in1=whole, op=ALU.subtract)
+        frac_c = const.tile([P, NCH * HALF], F32, name="frac_c")
+        nc.vector.tensor_scalar(out=frac_c, in0=frac, scalar1=0.25, scalar2=None, op0=ALU.add)
+        neg_s = const.tile([P, NCH * HALF], F32, name="neg_s")
+        nc.vector.scalar_tensor_tensor(out=neg_s, in0=frac, scalar=0.5, in1=frac, op0=ALU.is_gt, op1=ALU.subtract)
+        neg_c = const.tile([P, NCH * HALF], F32, name="neg_c")
+        nc.vector.scalar_tensor_tensor(out=neg_c, in0=frac_c, scalar=0.5, in1=frac_c, op0=ALU.is_gt, op1=ALU.subtract)
+        cc = const.tile([P, NCH * HALF, 2], F32, name="cc")
+        ss = const.tile([P, NCH * HALF, 2], F32, name="ss")
+        nc.scalar.activation(out=ss[:, :, 0], in_=neg_s, func=ACT.Sin, scale=TWO_PI)
+        nc.scalar.activation(out=ss[:, :, 1], in_=neg_s, func=ACT.Sin, scale=-TWO_PI)
+        nc.scalar.activation(out=cc[:, :, 0], in_=neg_c, func=ACT.Sin, scale=-TWO_PI)
+        nc.scalar.activation(out=cc[:, :, 1], in_=neg_c, func=ACT.Sin, scale=-TWO_PI)
+        warm = const.tile([P, 2], F32, name="warm")
+        nc.scalar.activation(out=warm, in_=cc[:, 0, :], func=ACT.Exp, scale=0.0)
+
+        wgrp = const.tile([P, 2, 512, 4], BF16, name="wgrp", align_bytes=64)
+        wcodes = const.tile([P, 1024], U32, name="wcodes", align_bytes=64)
+        wscales = const.tile([P, 1024], U8, name="wscales", align_bytes=64)
+
+        def interleave_w(key, m, g):
+            nc.scalar.copy(out=wgrp[:, g, m * 256:(m + 1) * 256, :], in_=wraw[key][:, g].rearrange("p j n -> p n j"))
+
+        def quantize_w():
+            nc.vector.quantize_mx(out=wcodes.bitcast(FP8X4), scales=wscales, in_=wgrp.rearrange("p g n j -> p (g n j)"))
+
+        xb = {}
+        xt = {}
+        grp = {}
+        hcodes = {}
+        hscales = {}
+        acc = {}
+
+        def widen(i):
+            xb[i] = xb_pool.tile([P, HID], BF16, name="xb")
+            nc.vector.tensor_tensor(out=xb[i], in0=hb[i].bitcast(FP8), in1=scale_bc, op=ALU.mult)
+
+        def turn(i):
+            words = xb[i].bitcast(F32)
+            xt[i] = ps_xt.tile([P, 4, P], F32, name="xt")
+            for g in range(2):
+                for u in range(2):
+                    nc.tensor.transpose(xt[i][:, 2 * g + u, :], words[:, 256 * g + u:256 * (g + 1):2], ident)
+
+        def gather(i):
+            r, c = divmod(i, NCH)
+            h, cl = divmod(c, NCH // PARTS[r])
+            if c == 0:
+                grp[r] = grp_pool.tile([P, 4 * HID], BF16, name="grp", align_bytes=64)
+            gw = grp[r].bitcast(F32).rearrange("p (h g x) -> p h g x", h=PARTS[r], g=2)
+            nc.scalar.copy(
+                out=gw[:, h, :, 256 * cl:256 * (cl + 1)].rearrange("p g (w u) -> p g w u", u=2),
+                in_=xt[i].rearrange("p (g u) w -> p g w u", u=2),
+            )
+
+        def quantize_hidden(r, h):
+            if h == 0:
+                hcodes[r] = code_pool.tile([P, 1024], U32, name="hcodes", align_bytes=64)
+                hscales[r] = code_pool.tile([P, 1024], U8, name="hscales", align_bytes=64)
+            n = 1024 // PARTS[r]
+            nc.vector.quantize_mx(
+                out=hcodes[r][:, h * n:(h + 1) * n].bitcast(FP8X4),
+                scales=hscales[r][:, h * n:(h + 1) * n],
+                in_=grp[r][:, 4 * h * n:4 * (h + 1) * n],
+            )
+
+        def project(r, h, kind, his):
+            wd = NW // PARTS[r]
+            dst = {}
+            for hi in his:
+                bank, off = divmod(((h * 2 + kind) * 2 + hi) * wd, NW)
+                if off == 0:
+                    acc[bank] = ps_mx.tile([P, NW], F32, name="acc%d" % bank)
+                dst[hi] = acc[bank][:, off:off + wd]
+                m = 2 * kind + hi
+                for g in range(2):
+                    wc = slice(g * 512 + m * P, g * 512 + (m + 1) * P)
+                    hc = slice((h * 2 + g) * wd, (h * 2 + g + 1) * wd)
+                    nc.tensor.matmul_mx(
+                        out=dst[hi],
+                        lhsT=wcodes[:, wc].bitcast(FP8X4), lhsT_scale=wscales[:, wc],
+                        rhs=hcodes[r][:, hc].bitcast(FP8X4), rhs_scale=hscales[r][:, hc],
+                        start=(g == 0), stop=(g == 1),
+                    )
+            for hi in his:
+                s = 4 * hi + r
+                cols = slice(1 - hi + h * wd, 1 - hi + (h + 1) * wd)
+                if kind == GATE:
+                    nc.scalar.activation(out=g8[:, s, cols], in_=dst[hi], func=ACT.Identity, bias=ape_t[:, s:s + 1], scale=1.0)
+                else:
+                    nc.scalar.copy(out=kv8[:, s, cols], in_=dst[hi])
+
+        gmax = const.tile([P, NW], F32, name="gmax")
+
+        def first_max():
+            nc.vector.tensor_tensor(out=gmax, in0=g8[:, 0, 0:NW], in1=g8[:, 4, 0:NW], op=ALU.max)
+
+        def run_max(s, c0, c1):
+            nc.vector.tensor_tensor(out=gmax[:, c0:c1], in0=gmax[:, c0:c1], in1=g8[:, s, c0:c1], op=ALU.max)
+
+        e8 = {}
+        p8 = {}
+        zt = {}
+        at = {}
+        rz = {}
+        o1 = {}
+        o0 = {}
+        t1 = {}
+        t2 = {}
+
+        def shift(c):
+            cols = slice(c * P, (c + 1) * P)
+            e8[c] = fin_pool.tile([P, 8, P], F32, name="e8")
+            nc.vector.tensor_tensor(out=e8[c], in0=g8[:, :, cols], in1=gmax[:, cols].unsqueeze(1).to_broadcast([P, 8, P]), op=ALU.subtract)
+            nc.scalar.activation(out=e8[c], in_=e8[c], func=ACT.Exp)
+
+        def sum_z(c):
+            zt[c] = ps_xt.tile([P, P], F32, name="xt")
+            for s in range(8):
+                nc.tensor.matmul(out=zt[c], lhsT=e8[c][:, s, :], rhs=ident, is_transpose=True, start=(s == 0), stop=(s == 7))
+
+        def weigh(c):
+            cols = slice(c * P, (c + 1) * P)
+            p8[c] = fin_pool.tile([P, 8, P], F32, name="p8")
+            nc.vector.tensor_tensor(out=p8[c], in0=e8[c], in1=kv8[:, :, cols], op=ALU.mult)
+            at[c] = ps_mx.tile([P, P], F32, name="acc%d" % c)
+            for s in range(8):
+                nc.tensor.matmul(out=at[c], lhsT=p8[c][:, s, :], rhs=ident, is_transpose=True, start=(s == 0), stop=(s == 7))
+
+        def recip(c):
+            rz[c] = fin_pool.tile([P, P], F32, name="rz")
+            nc.vector.reciprocal(out=rz[c], in_=zt[c])
+
+        def norm(c):
+            o1[c] = fin_pool.tile([P, P], F32, name="o1")
+            nc.vector.tensor_tensor(out=o1[c], in0=at[c], in1=rz[c], op=ALU.mult)
+            nc.sync.dma_start(out=o1_view[c], in_=o1[c])
+            o0[c] = fin_pool.tile([P, P], F32, name="o0")
+            nc.scalar.copy(out=o0[c][:, 0:64], in_=o1[c][:, 0:64])
+
+        def rot_mul(c):
+            rot = o1[c][:, 64:128].rearrange("p (j e) -> p j e", e=2)
+            tj = slice(c * HALF, (c + 1) * HALF)
+            t1[c] = fin_pool.tile([P, HALF, 2], F32, name="t1")
+            t2[c] = fin_pool.tile([P, HALF, 2], F32, name="t2")
+            nc.vector.tensor_tensor(out=t1[c], in0=rot, in1=cc[:, tj, :], op=ALU.mult)
+            nc.vector.tensor_tensor(out=t2[c], in0=rot[:, :, ::-1], in1=ss[:, tj, :], op=ALU.mult)
+
+        def rot_add(c):
+            nc.vector.tensor_tensor(out=o0[c][:, 64:128].rearrange("p (j e) -> p j e", e=2), in0=t1[c], in1=t2[c], op=ALU.add)
+            nc.sync.dma_start(out=o0_view[c], in_=o0[c])
+
+        w_piece = {0: ("gate", 0, 0), 1: ("gate", 0, 1), 3: ("kv", 1, 0), 5: ("kv", 1, 1)}
+        for i in range(RATIO * NCH):
+            widen(i)
+            turn(i)
+            gather(i)
+            if i in w_piece:
+                interleave_w(*w_piece[i])
+            if i == 5:
+                quantize_hidden(0, 0)
+            if i == 7:
+                quantize_w()
+                project(0, 0, GATE, (0, 1))
+            if i == 8:
+                project(0, 0, KV, (0, 1))
+            if i == 9:
+                quantize_hidden(1, 0)
+                project(1, 0, GATE, (0,))
+            if i == 10:
+                project(1, 0, GATE, (1,))
+                first_max()
+            if i == 11:
+                project(1, 0, KV, (0,))
+                run_max(1, 0, NW)
+            if i == 12:
+                project(1, 0, KV, (1,))
+                run_max(5, 0, NW)
+            if i == 13:
+                quantize_hidden(2, 0)
+                project(2, 0, GATE, (0,))
+            if i == 14:
+                project(2, 0, GATE, (1,))
+            if i == 15:
+                project(2, 0, KV, (0,))
+        run_max(2, 0, NW)
+        quantize_hidden(3, 0)
+        project(3, 0, GATE, (0, 1))
+        project(2, 0, KV, (1,))
+        run_max(6, 0, NW)
+        quantize_hidden(3, 1)
+        project(3, 1, GATE, (0, 1))
+        project(3, 0, KV, (0, 1))
+        project(3, 1, KV, (0, 1))
+        run_max(3, 0, 256)
+        run_max(7, 0, 256)
+        shift(0)
+        shift(1)
+        sum_z(0)
+        run_max(3, 256, NW)
+        weigh(0)
+        sum_z(1)
+        run_max(7, 256, NW)
+        weigh(1)
+        shift(2)
+        recip(0)
+        shift(3)
+        sum_z(2)
+        norm(0)
+        weigh(2)
+        sum_z(3)
+        rot_mul(0)
+        recip(1)
+        weigh(3)
+        rot_add(0)
+        norm(1)
+        recip(2)
+        rot_mul(1)
+        recip(3)
+        norm(2)
+        rot_add(1)
+        rot_mul(2)
+        norm(3)
+        rot_add(2)
+        rot_mul(3)
+        rot_add(3)

@@ -198,8 +198,16 @@ def tile_deepseekv4attention_pa_kernel(tc, hidden_bytes, hidden_scale, wkv, wgat
 
         gmax = const.tile([P, NW], F32, name="gmax")
 
-        def first_max():
-            nc.vector.tensor_tensor(out=gmax, in0=g8[:, 0, 0:NW], in1=g8[:, 4, 0:NW], op=ALU.max)
+        hmax = const.tile([P, NW], F32, name="hmax")
+
+        def pair_max(dst, s):
+            nc.vector.tensor_tensor(out=dst, in0=g8[:, s, 0:NW], in1=g8[:, s + 1, 0:NW], op=ALU.max)
+
+        def more_max(dst, s):
+            nc.vector.tensor_tensor(out=dst, in0=dst, in1=g8[:, s, 0:NW], op=ALU.max)
+
+        def join_max():
+            nc.vector.tensor_tensor(out=gmax, in0=gmax, in1=hmax, op=ALU.max)
 
         def run_max(s, c0, c1):
             nc.vector.tensor_tensor(out=gmax[:, c0:c1], in0=gmax[:, c0:c1], in1=g8[:, s, c0:c1], op=ALU.max)
@@ -275,13 +283,10 @@ def tile_deepseekv4attention_pa_kernel(tc, hidden_bytes, hidden_scale, wkv, wgat
                 project(1, 0, GATE, (0,))
             if i == 10:
                 project(1, 0, GATE, (1,))
-                first_max()
             if i == 11:
                 project(1, 0, KV, (0,))
-                run_max(1, 0, NW)
             if i == 12:
                 project(1, 0, KV, (1,))
-                run_max(5, 0, NW)
             if i == 13:
                 quantize_hidden(2, 0)
                 project(2, 0, GATE, (0,))
@@ -289,12 +294,15 @@ def tile_deepseekv4attention_pa_kernel(tc, hidden_bytes, hidden_scale, wkv, wgat
                 project(2, 0, GATE, (1,))
             if i == 15:
                 project(2, 0, KV, (0,))
-        run_max(2, 0, NW)
         quantize_hidden(3, 0)
         project(3, 0, GATE, (0, 1))
         project(2, 0, KV, (1,))
-        run_max(6, 0, NW)
+        pair_max(gmax, 0)
+        pair_max(hmax, 4)
+        more_max(gmax, 2)
+        more_max(hmax, 6)
         quantize_hidden(3, 1)
+        join_max()
         project(3, 1, GATE, (0, 1))
         project(3, 0, KV, (0, 1))
         project(3, 1, KV, (0, 1))

@@ -47,8 +47,9 @@ def tile_deepseekv4attention_pa_kernel(tc, hidden_bytes, hidden_scale, wkv, wgat
         ps_mx = ctx.enter_context(tc.psum_pool(name="ps_mx", bufs=1))
         ctx.enter_context(tc.manual_schedule())
 
+        scale_col = const.tile([P, 8], F32, name="scale_col")
+        nc.scalar.dma_start(out=scale_col, in_=hidden_scale.rearrange("a b (p j) -> (a b p) j", j=8))
         scale_bc = const.tile([P, HID], F32, name="scale_bc")
-        nc.scalar.dma_start(out=scale_bc, in_=hidden_scale.rearrange("a b k -> (a b k)").partition_broadcast(P))
         hb = {}
 
         def load_bytes(i):
@@ -82,6 +83,15 @@ def tile_deepseekv4attention_pa_kernel(tc, hidden_bytes, hidden_scale, wkv, wgat
         nc.gpsimd.iota(pos_i, pattern=[[RATIO * P, NCH]], base=0, channel_multiplier=RATIO)
         ident = const.tile([P, P], F32, name="ident")
         make_identity(nc, ident)
+        by_j = scale_bc.rearrange("p (n j) -> p n j", j=8)
+        spread = {}
+        for h in range(2):
+            spread[h] = ps_xt.tile([P, 4, P], F32, name="xt")
+            for j in range(4):
+                nc.tensor.matmul(out=spread[h][:, j, :], lhsT=scale_col[:, 4 * h + j:4 * h + j + 1].to_broadcast([P, P]), rhs=ident, is_transpose=True, start=True, stop=True)
+        first = const.tile([P, 2], F32, name="first")
+        nc.scalar.activation(out=first, in_=ident[:, 0:2], func=ACT.Sin, scale=0.0)
+        nc.scalar.copy(out=by_j[:, :, 0:4], in_=spread[0].rearrange("p j n -> p n j"))
         g8 = const.tile([P, 8, GW], F32, name="g8")
         kv8 = const.tile([P, 8, GW], F32, name="kv8")
         nc.gpsimd.memset(g8[:, 0:4, 0:1], -1.0e30)
@@ -111,6 +121,7 @@ def tile_deepseekv4attention_pa_kernel(tc, hidden_bytes, hidden_scale, wkv, wgat
         nc.vector.scalar_tensor_tensor(out=neg_s, in0=frac, scalar=0.5, in1=frac, op0=ALU.is_gt, op1=ALU.subtract)
         neg_c = const.tile([P, NCH * HALF], F32, name="neg_c")
         nc.vector.scalar_tensor_tensor(out=neg_c, in0=frac_c, scalar=0.5, in1=frac_c, op0=ALU.is_gt, op1=ALU.subtract)
+        nc.vector.tensor_copy(out=by_j[:, :, 4:8], in_=spread[1].rearrange("p j n -> p n j"))
         cc = const.tile([P, NCH * HALF, 2], F32, name="cc")
         ss = const.tile([P, NCH * HALF, 2], F32, name="ss")
         nc.scalar.activation(out=ss[:, :, 0], in_=neg_s, func=ACT.Sin, scale=TWO_PI)

@@ -314,26 +314,26 @@ def tile_deepseekv4attention_pa_kernel(tc, hidden_bytes, hidden_scale, wkv, wgat
         more_max(hmax, 6)
         quantize_hidden(3, 1)
         join_max()
-        project(3, 1, GATE, (0, 1))
         project(3, 0, KV, (0, 1))
-        project(3, 1, KV, (0, 1))
+        project(3, 1, GATE, (0, 1))
         run_max(3, 0, 256)
         run_max(7, 0, 256)
         shift(0)
-        shift(1)
-        sum_z(0)
         run_max(3, 256, NW)
+        shift(1)
+        project(3, 1, KV, (0, 1))
+        sum_z(0)
+        run_max(7, 256, NW)
         weigh(0)
         sum_z(1)
-        run_max(7, 256, NW)
-        weigh(1)
         shift(2)
-        recip(0)
+        weigh(1)
         shift(3)
         sum_z(2)
-        norm(0)
+        recip(0)
         weigh(2)
         sum_z(3)
+        norm(0)
         rot_mul(0)
         recip(1)
         weigh(3)

@@ -47,8 +47,8 @@ def tile_deepseekv4attention_pa_kernel(tc, hidden_bytes, hidden_scale, wkv, wgat
         ps_mx = ctx.enter_context(tc.psum_pool(name="ps_mx", bufs=1))
         ctx.enter_context(tc.manual_schedule())
 
-        scale_col = const.tile([P, 8], F32, name="scale_col")
-        nc.scalar.dma_start(out=scale_col, in_=hidden_scale.rearrange("a b (p j) -> (a b p) j", j=8))
+        scale_col = const.tile([P, 2, 4], F32, name="scale_col")
+        nc.sync.dma_start(out=scale_col, in_=hidden_scale.rearrange("a b (h p j) -> (a b p) h j", h=2, j=4))
         scale_bc = const.tile([P, HID], F32, name="scale_bc")
         hb = {}
 
@@ -69,29 +69,28 @@ def tile_deepseekv4attention_pa_kernel(tc, hidden_bytes, hidden_scale, wkv, wgat
         load_bytes(2)
         load_w("gate", wgate)
         load_w("kv", wkv)
-        for i in range(3, RATIO * NCH):
+        for i in range(3, 8):
             load_bytes(i)
-
         ape_b = []
         with nc.allow_non_contiguous_dma(reason="ape: 1024 values, one feature to a partition"):
             for h in range(2):
                 t = const.tile([P, RATIO], BF16, name="ape_b%d" % h)
-                nc.scalar.dma_start(out=t, in_=ape[:, h * P:(h + 1) * P].rearrange("r f -> f r"))
+                nc.sync.dma_start(out=t, in_=ape[:, h * P:(h + 1) * P].rearrange("r f -> f r"))
                 ape_b.append(t)
+        for i in range(8, RATIO * NCH):
+            load_bytes(i)
 
         pos_i = const.tile([P, NCH], I32, name="pos_i")
         nc.gpsimd.iota(pos_i, pattern=[[RATIO * P, NCH]], base=0, channel_multiplier=RATIO)
         ident = const.tile([P, P], F32, name="ident")
         make_identity(nc, ident)
-        by_j = scale_bc.rearrange("p (n j) -> p n j", j=8)
-        spread = {}
-        for h in range(2):
-            spread[h] = ps_xt.tile([P, 4, P], F32, name="xt")
-            for j in range(4):
-                nc.tensor.matmul(out=spread[h][:, j, :], lhsT=scale_col[:, 4 * h + j:4 * h + j + 1].to_broadcast([P, P]), rhs=ident, is_transpose=True, start=True, stop=True)
         first = const.tile([P, 2], F32, name="first")
         nc.scalar.activation(out=first, in_=ident[:, 0:2], func=ACT.Sin, scale=0.0)
-        nc.scalar.copy(out=by_j[:, :, 0:4], in_=spread[0].rearrange("p j n -> p n j"))
+        for h in range(2):
+            spread = ps_xt.tile([P, 4, P], F32, name="xt")
+            for j in range(4):
+                nc.tensor.matmul(out=spread[:, j, :], lhsT=scale_col[:, h, j:j + 1].to_broadcast([P, P]), rhs=ident, is_transpose=True, start=True, stop=True)
+            nc.scalar.copy(out=scale_bc[:, 512 * h:512 * (h + 1)].rearrange("p (n j) -> p n j", j=4), in_=spread.rearrange("p j n -> p n j"))
         g8 = const.tile([P, 8, GW], F32, name="g8")
         kv8 = const.tile([P, 8, GW], F32, name="kv8")
         nc.gpsimd.memset(g8[:, 0:4, 0:1], -1.0e30)
@@ -121,7 +120,6 @@ def tile_deepseekv4attention_pa_kernel(tc, hidden_bytes, hidden_scale, wkv, wgat
         nc.vector.scalar_tensor_tensor(out=neg_s, in0=frac, scalar=0.5, in1=frac, op0=ALU.is_gt, op1=ALU.subtract)
         neg_c = const.tile([P, NCH * HALF], F32, name="neg_c")
         nc.vector.scalar_tensor_tensor(out=neg_c, in0=frac_c, scalar=0.5, in1=frac_c, op0=ALU.is_gt, op1=ALU.subtract)
-        nc.vector.tensor_copy(out=by_j[:, :, 4:8], in_=spread[1].rearrange("p j n -> p n j"))
         cc = const.tile([P, NCH * HALF, 2], F32, name="cc")
         ss = const.tile([P, NCH * HALF, 2], F32, name="ss")
         nc.scalar.activation(out=ss[:, :, 0], in_=neg_s, func=ACT.Sin, scale=TWO_PI)
@@ -150,7 +148,12 @@ def tile_deepseekv4attention_pa_kernel(tc, hidden_bytes, hidden_scale, wkv, wgat
 
         def widen(i):
             xb[i] = xb_pool.tile([P, HID], BF16, name="xb")
-            nc.vector.tensor_tensor(out=xb[i], in0=hb[i].bitcast(FP8), in1=scale_bc, op=ALU.mult)
+            if i == 0:
+                for h in range(2):
+                    half = slice(512 * h, 512 * (h + 1))
+                    nc.vector.tensor_tensor(out=xb[i][:, half], in0=hb[i][:, half].bitcast(FP8), in1=scale_bc[:, half], op=ALU.mult)
+            else:
+                nc.vector.tensor_tensor(out=xb[i], in0=hb[i].bitcast(FP8), in1=scale_bc, op=ALU.mult)
 
         def turn(i):
             words = xb[i].bitcast(F32)
@@ -282,29 +285,28 @@ def tile_deepseekv4attention_pa_kernel(tc, hidden_bytes, hidden_scale, wkv, wgat
             gather(i)
             if i in w_piece:
                 interleave_w(*w_piece[i])
-            if i == 5:
+            if i == 6:
                 quantize_hidden(0, 0)
-            if i == 7:
+            if i == 8:
                 quantize_w()
                 project(0, 0, GATE, (0, 1))
-            if i == 8:
-                project(0, 0, KV, (0, 1))
             if i == 9:
+                project(0, 0, KV, (0, 1))
+            if i == 10:
                 quantize_hidden(1, 0)
                 project(1, 0, GATE, (0,))
-            if i == 10:
-                project(1, 0, GATE, (1,))
             if i == 11:
-                project(1, 0, KV, (0,))
+                project(1, 0, GATE, (1,))
             if i == 12:
-                project(1, 0, KV, (1,))
+                project(1, 0, KV, (0,))
             if i == 13:
+                project(1, 0, KV, (1,))
+            if i == 14:
                 quantize_hidden(2, 0)
                 project(2, 0, GATE, (0,))
-            if i == 14:
-                project(2, 0, GATE, (1,))
             if i == 15:
-                project(2, 0, KV, (0,))
+                project(2, 0, GATE, (1,))
+        project(2, 0, KV, (0,))
         quantize_hidden(3, 0)
         project(3, 0, GATE, (0, 1))
         project(2, 0, KV, (1,))

@@ -310,13 +310,13 @@ def tile_deepseekv4attention_pa_kernel(tc, hidden_bytes, hidden_scale, wkv, wgat
         quantize_hidden(3, 0)
         project(3, 0, GATE, (0, 1))
         project(2, 0, KV, (1,))
+        project(3, 0, KV, (0, 1))
         pair_max(gmax, 0)
         pair_max(hmax, 4)
         more_max(gmax, 2)
         more_max(hmax, 6)
         quantize_hidden(3, 1)
         join_max()
-        project(3, 0, KV, (0, 1))
         project(3, 1, GATE, (0, 1))
         run_max(3, 0, 256)
         run_max(7, 0, 256)

@@ -21,40 +21,40 @@ HID = 1024
 NW = 512
 RATIO = 4
 NCH = 4
+NT = RATIO * NCH
 HALF = 32
 THETA = 10000.0
 GW = 520
 TWO_PI = 2.0 * math.pi
-PARTS = (1, 1, 1, 2)
-GATE = 0
-KV = 1
+LEAD = 3
+VCAST = (2, 3)
 
 
 def tile_deepseekv4attention_pa_kernel(tc, hidden_bytes, hidden_scale, wkv, wgate, ape, out_0, out_1):
     nc = tc.nc
-    hb_view = hidden_bytes.rearrange("o (c w r) k -> o r c w k", c=NCH, w=P, r=RATIO)[0]
+    hb_view = hidden_bytes.rearrange("o (c w r) k -> o c r w k", c=NCH, w=P, r=RATIO)[0]
     o0_view = out_0.rearrange("o (c p) f -> o c p f", p=P)[0]
     o1_view = out_1.rearrange("o (c p) f -> o c p f", p=P)[0]
 
     with ExitStack() as ctx:
         const = ctx.enter_context(tc.tile_pool(name="const", bufs=1))
         bytes_pool = ctx.enter_context(tc.tile_pool(name="bytes", bufs=1))
-        xb_pool = ctx.enter_context(tc.tile_pool(name="xb", bufs=6))
+        xb_pool = ctx.enter_context(tc.tile_pool(name="xb", bufs=5))
         grp_pool = ctx.enter_context(tc.tile_pool(name="grp", bufs=2))
         code_pool = ctx.enter_context(tc.tile_pool(name="codes", bufs=2))
-        fin_pool = ctx.enter_context(tc.tile_pool(name="fin", bufs=4))
-        ps_xt = ctx.enter_context(tc.psum_pool(name="ps_xt", bufs=4))
+        fin_pool = ctx.enter_context(tc.tile_pool(name="fin", bufs=2))
+        ps_xt = ctx.enter_context(tc.psum_pool(name="ps_xt", bufs=2))
         ps_mx = ctx.enter_context(tc.psum_pool(name="ps_mx", bufs=1))
+        ps_sum = ctx.enter_context(tc.psum_pool(name="ps_sum", bufs=1))
         ctx.enter_context(tc.manual_schedule())
 
         scale_col = const.tile([P, 2, 4], F32, name="scale_col")
-        nc.sync.dma_start(out=scale_col, in_=hidden_scale.rearrange("a b (h p j) -> (a b p) h j", h=2, j=4))
-        scale_bc = const.tile([P, HID], F32, name="scale_bc")
+        nc.sync.dma_start(out=scale_col, in_=hidden_scale.rearrange("a b (g p t) -> (a b p) g t", g=2, t=4))
         hb = {}
 
         def load_bytes(i):
             t = bytes_pool.tile([P, HID], U8, name="hb_%d" % i)
-            nc.sync.dma_start(out=t, in_=hb_view[i // NCH, i % NCH])
+            nc.sync.dma_start(out=t, in_=hb_view[i // RATIO, i % RATIO])
             hb[i] = t
 
         wraw = {}
@@ -64,12 +64,11 @@ def tile_deepseekv4attention_pa_kernel(tc, hidden_bytes, hidden_scale, wkv, wgat
             nc.sync.dma_start(out=t, in_=w.rearrange("(g p j) n -> p g j n", g=2, p=P, j=4))
             wraw[key] = t
 
-        load_bytes(0)
-        load_bytes(1)
-        load_bytes(2)
+        for i in range(4):
+            load_bytes(i)
         load_w("gate", wgate)
         load_w("kv", wkv)
-        for i in range(3, 8):
+        for i in range(4, 8):
             load_bytes(i)
         ape_b = []
         with nc.allow_non_contiguous_dma(reason="ape: 1024 values, one feature to a partition"):
@@ -77,7 +76,7 @@ def tile_deepseekv4attention_pa_kernel(tc, hidden_bytes, hidden_scale, wkv, wgat
                 t = const.tile([P, RATIO], BF16, name="ape_b%d" % h)
                 nc.sync.dma_start(out=t, in_=ape[:, h * P:(h + 1) * P].rearrange("r f -> f r"))
                 ape_b.append(t)
-        for i in range(8, RATIO * NCH):
+        for i in range(8, NT):
             load_bytes(i)
 
         pos_i = const.tile([P, NCH], I32, name="pos_i")
@@ -86,18 +85,10 @@ def tile_deepseekv4attention_pa_kernel(tc, hidden_bytes, hidden_scale, wkv, wgat
         make_identity(nc, ident)
         first = const.tile([P, 2], F32, name="first")
         nc.scalar.activation(out=first, in_=ident[:, 0:2], func=ACT.Sin, scale=0.0)
-        for h in range(2):
-            spread = ps_xt.tile([P, 4, P], F32, name="xt")
-            for j in range(4):
-                nc.tensor.matmul(out=spread[:, j, :], lhsT=scale_col[:, h, j:j + 1].to_broadcast([P, P]), rhs=ident, is_transpose=True, start=True, stop=True)
-            nc.scalar.copy(out=scale_bc[:, 512 * h:512 * (h + 1)].rearrange("p (n j) -> p n j", j=4), in_=spread.rearrange("p j n -> p n j"))
         g8 = const.tile([P, 8, GW], F32, name="g8")
-        kv8 = const.tile([P, 8, GW], F32, name="kv8")
+        kv4 = const.tile([P, 4, GW], F32, name="kv4")
         nc.gpsimd.memset(g8[:, 0:4, 0:1], -1.0e30)
-        nc.gpsimd.memset(kv8[:, 0:4, 0:1], 0.0)
-        ape_t = const.tile([P, 8], F32, name="ape_t")
-        for h in range(2):
-            nc.gpsimd.tensor_copy(out=ape_t[:, 4 * h:4 * h + 4], in_=ape_b[h])
+        nc.gpsimd.memset(kv4[:, :, 0:1], 0.0)
 
         pos = const.tile([P, NCH], F32, name="pos")
         nc.vector.tensor_copy(out=pos, in_=pos_i)
@@ -122,22 +113,33 @@ def tile_deepseekv4attention_pa_kernel(tc, hidden_bytes, hidden_scale, wkv, wgat
         nc.vector.scalar_tensor_tensor(out=neg_c, in0=frac_c, scalar=0.5, in1=frac_c, op0=ALU.is_gt, op1=ALU.subtract)
         cc = const.tile([P, NCH * HALF, 2], F32, name="cc")
         ss = const.tile([P, NCH * HALF, 2], F32, name="ss")
-        nc.scalar.activation(out=ss[:, :, 0], in_=neg_s, func=ACT.Sin, scale=TWO_PI)
-        nc.scalar.activation(out=ss[:, :, 1], in_=neg_s, func=ACT.Sin, scale=-TWO_PI)
-        nc.scalar.activation(out=cc[:, :, 0], in_=neg_c, func=ACT.Sin, scale=-TWO_PI)
-        nc.scalar.activation(out=cc[:, :, 1], in_=neg_c, func=ACT.Sin, scale=-TWO_PI)
-        warm = const.tile([P, 2], F32, name="warm")
-        nc.scalar.activation(out=warm, in_=cc[:, 0, :], func=ACT.Exp, scale=0.0)
 
-        wgrp = const.tile([P, 2, 512, 4], BF16, name="wgrp", align_bytes=64)
+        def sin_tables():
+            nc.scalar.activation(out=ss[:, :, 0], in_=neg_s, func=ACT.Sin, scale=TWO_PI)
+            nc.scalar.activation(out=ss[:, :, 1], in_=neg_s, func=ACT.Sin, scale=-TWO_PI)
+            nc.scalar.activation(out=cc[:, :, 0], in_=neg_c, func=ACT.Sin, scale=-TWO_PI)
+            nc.scalar.activation(out=cc[:, :, 1], in_=neg_c, func=ACT.Sin, scale=-TWO_PI)
+            warm = const.tile([P, 2], F32, name="warm")
+            nc.scalar.activation(out=warm, in_=cc[:, 0, :], func=ACT.Exp, scale=0.0)
+
+        wgrp = const.tile([P, 2, 2, 256, 4], BF16, name="wgrp", align_bytes=64)
         wcodes = const.tile([P, 1024], U32, name="wcodes", align_bytes=64)
         wscales = const.tile([P, 1024], U8, name="wscales", align_bytes=64)
+        KEYS = ("gate", "kv")
 
-        def interleave_w(key, m, g):
-            nc.scalar.copy(out=wgrp[:, g, m * 256:(m + 1) * 256, :], in_=wraw[key][:, g].rearrange("p j n -> p n j"))
+        def interleave_w(kind, g):
+            nc.gpsimd.tensor_scalar(out=wgrp[:, kind, g], in0=wraw[KEYS[kind]][:, g].rearrange("p j n -> p n j"), scalar1=1.0, scalar2=0.0, op0=ALU.mult, op1=ALU.add)
 
-        def quantize_w():
-            nc.vector.quantize_mx(out=wcodes.bitcast(FP8X4), scales=wscales, in_=wgrp.rearrange("p g n j -> p (g n j)"))
+        def quantize_w(kind):
+            cols = slice(512 * kind, 512 * (kind + 1))
+            nc.vector.quantize_mx(out=wcodes[:, cols].bitcast(FP8X4), scales=wscales[:, cols], in_=wgrp[:, kind].rearrange("p g n j -> p (g n j)"))
+
+        for kind in range(2):
+            for g in range(2):
+                interleave_w(kind, g)
+        ape_t = const.tile([P, 8], F32, name="ape_t")
+        for h in range(2):
+            nc.gpsimd.tensor_copy(out=ape_t[:, 4 * h:4 * h + 4], in_=ape_b[h])
 
         xb = {}
         xt = {}
@@ -146,86 +148,64 @@ def tile_deepseekv4attention_pa_kernel(tc, hidden_bytes, hidden_scale, wkv, wgat
         hscales = {}
         acc = {}
 
-        def widen(i):
+        def cast(i):
             xb[i] = xb_pool.tile([P, HID], BF16, name="xb")
-            if i == 0:
-                for h in range(2):
-                    half = slice(512 * h, 512 * (h + 1))
-                    nc.vector.tensor_tensor(out=xb[i][:, half], in0=hb[i][:, half].bitcast(FP8), in1=scale_bc[:, half], op=ALU.mult)
+            if i in VCAST:
+                nc.vector.tensor_copy(out=xb[i], in_=hb[i].bitcast(FP8))
             else:
-                nc.vector.tensor_tensor(out=xb[i], in0=hb[i].bitcast(FP8), in1=scale_bc, op=ALU.mult)
+                nc.scalar.copy(out=xb[i], in_=hb[i].bitcast(FP8))
 
         def turn(i):
             words = xb[i].bitcast(F32)
-            xt[i] = ps_xt.tile([P, 4, P], F32, name="xt")
+            xt[i] = ps_xt.tile([P, 2, 2, P], F32, name="xt")
             for g in range(2):
                 for u in range(2):
-                    nc.tensor.transpose(xt[i][:, 2 * g + u, :], words[:, 256 * g + u:256 * (g + 1):2], ident)
+                    nc.tensor.transpose(xt[i][:, u, g, :], words[:, 256 * g + u:256 * (g + 1):2], ident)
 
-        def gather(i):
-            r, c = divmod(i, NCH)
-            h, cl = divmod(c, NCH // PARTS[r])
-            if c == 0:
-                grp[r] = grp_pool.tile([P, 4 * HID], BF16, name="grp", align_bytes=64)
-            gw = grp[r].bitcast(F32).rearrange("p (h g x) -> p h g x", h=PARTS[r], g=2)
-            nc.scalar.copy(
-                out=gw[:, h, :, 256 * cl:256 * (cl + 1)].rearrange("p g (w u) -> p g w u", u=2),
-                in_=xt[i].rearrange("p (g u) w -> p g w u", u=2),
+        def mult(i):
+            c, r = divmod(i, RATIO)
+            if r == 0:
+                grp[c] = grp_pool.tile([P, 4 * HID], BF16, name="grp", align_bytes=64)
+            nc.vector.tensor_tensor(
+                out=grp[c].rearrange("p (g r x) -> p g r x", g=2, r=RATIO)[:, :, r, :].rearrange("p g (w u e) -> p g w u e", u=2, e=2),
+                in0=xt[i].rearrange("p u g w -> p (u g w)").bitcast(BF16).rearrange("p (u g w e) -> p g w u e", u=2, g=2, e=2),
+                in1=scale_col.rearrange("p g (u e) -> p g u e", e=2).unsqueeze(2).to_broadcast([P, 2, P, 2, 2]),
+                op=ALU.mult,
             )
 
-        def quantize_hidden(r, h):
-            if h == 0:
-                hcodes[r] = code_pool.tile([P, 1024], U32, name="hcodes", align_bytes=64)
-                hscales[r] = code_pool.tile([P, 1024], U8, name="hscales", align_bytes=64)
-            n = 1024 // PARTS[r]
-            nc.vector.quantize_mx(
-                out=hcodes[r][:, h * n:(h + 1) * n].bitcast(FP8X4),
-                scales=hscales[r][:, h * n:(h + 1) * n],
-                in_=grp[r][:, 4 * h * n:4 * (h + 1) * n],
-            )
+        def quantize_hidden(c):
+            hcodes[c] = code_pool.tile([P, 1024], U32, name="hcodes", align_bytes=64)
+            hscales[c] = code_pool.tile([P, 1024], U8, name="hscales", align_bytes=64)
+            nc.vector.quantize_mx(out=hcodes[c].bitcast(FP8X4), scales=hscales[c], in_=grp[c])
 
-        def project(r, h, kind, his):
-            wd = NW // PARTS[r]
-            dst = {}
-            for hi in his:
-                bank, off = divmod(((h * 2 + kind) * 2 + hi) * wd, NW)
-                if off == 0:
-                    acc[bank] = ps_mx.tile([P, NW], F32, name="acc%d" % bank)
-                dst[hi] = acc[bank][:, off:off + wd]
-                m = 2 * kind + hi
-                for g in range(2):
-                    wc = slice(g * 512 + m * P, g * 512 + (m + 1) * P)
-                    hc = slice((h * 2 + g) * wd, (h * 2 + g + 1) * wd)
-                    nc.tensor.matmul_mx(
-                        out=dst[hi],
-                        lhsT=wcodes[:, wc].bitcast(FP8X4), lhsT_scale=wscales[:, wc],
-                        rhs=hcodes[r][:, hc].bitcast(FP8X4), rhs_scale=hscales[r][:, hc],
-                        start=(g == 0), stop=(g == 1),
-                    )
-            for hi in his:
+        def project(c, m, pool=None):
+            kind, hi = divmod(m, 2)
+            if pool is None:
+                acc[c, m] = ps_mx.tile([P, NW], F32, name="acc%d" % m)
+            else:
+                acc[c, m] = pool.tile([P, NW], F32, name="xt")
+            for g in range(2):
+                wc = slice(512 * kind + 256 * g + P * hi, 512 * kind + 256 * g + P * (hi + 1))
+                hc = slice(512 * g, 512 * (g + 1))
+                nc.tensor.matmul_mx(
+                    out=acc[c, m],
+                    lhsT=wcodes[:, wc].bitcast(FP8X4), lhsT_scale=wscales[:, wc],
+                    rhs=hcodes[c][:, hc].bitcast(FP8X4), rhs_scale=hscales[c][:, hc],
+                    start=(g == 0), stop=(g == 1),
+                )
+
+        def evac_gate(c, hi):
+            for r in range(RATIO):
                 s = 4 * hi + r
-                cols = slice(1 - hi + h * wd, 1 - hi + (h + 1) * wd)
-                if kind == GATE:
-                    nc.scalar.activation(out=g8[:, s, cols], in_=dst[hi], func=ACT.Identity, bias=ape_t[:, s:s + 1], scale=1.0)
-                else:
-                    nc.scalar.copy(out=kv8[:, s, cols], in_=dst[hi])
+                cols = slice(1 - hi + c * P, 1 - hi + (c + 1) * P)
+                nc.scalar.activation(out=g8[:, s, cols], in_=acc[c, hi][:, r * P:(r + 1) * P], func=ACT.Identity, bias=ape_t[:, s:s + 1], scale=1.0)
 
-        gmax = const.tile([P, NW], F32, name="gmax")
+        def evac_kvlo(c):
+            nc.scalar.copy(out=kv4[:, :, 1 + c * P:1 + (c + 1) * P], in_=acc[c, 2].rearrange("p (r w) -> p r w", r=RATIO))
 
-        hmax = const.tile([P, NW], F32, name="hmax")
-
-        def pair_max(dst, s):
-            nc.vector.tensor_tensor(out=dst, in0=g8[:, s, 0:NW], in1=g8[:, s + 1, 0:NW], op=ALU.max)
-
-        def more_max(dst, s):
-            nc.vector.tensor_tensor(out=dst, in0=dst, in1=g8[:, s, 0:NW], op=ALU.max)
-
-        def join_max():
-            nc.vector.tensor_tensor(out=gmax, in0=gmax, in1=hmax, op=ALU.max)
-
-        def run_max(s, c0, c1):
-            nc.vector.tensor_tensor(out=gmax[:, c0:c1], in0=gmax[:, c0:c1], in1=g8[:, s, c0:c1], op=ALU.max)
-
+        m4 = {}
+        m2 = {}
+        gm = {}
         e8 = {}
         p8 = {}
         zt = {}
@@ -236,22 +216,45 @@ def tile_deepseekv4attention_pa_kernel(tc, hidden_bytes, hidden_scale, wkv, wgat
         t1 = {}
         t2 = {}
 
-        def shift(c):
+        def max1(c):
             cols = slice(c * P, (c + 1) * P)
-            e8[c] = fin_pool.tile([P, 8, P], F32, name="e8")
-            nc.vector.tensor_tensor(out=e8[c], in0=g8[:, :, cols], in1=gmax[:, cols].unsqueeze(1).to_broadcast([P, 8, P]), op=ALU.subtract)
-            nc.scalar.activation(out=e8[c], in_=e8[c], func=ACT.Exp)
+            m4[c] = fin_pool.tile([P, 4, P], F32, name="m4")
+            nc.vector.tensor_tensor(out=m4[c], in0=g8[:, 0:4, cols], in1=g8[:, 4:8, cols], op=ALU.max)
+
+        def max2(c):
+            m2[c] = fin_pool.tile([P, 2, P], F32, name="m2")
+            nc.vector.tensor_tensor(out=m2[c], in0=m4[c][:, 0:2, :], in1=m4[c][:, 2:4, :], op=ALU.max)
+
+        def max3(c):
+            gm[c] = fin_pool.tile([P, P], F32, name="gm")
+            nc.vector.tensor_tensor(out=gm[c], in0=m2[c][:, 0, :], in1=m2[c][:, 1, :], op=ALU.max)
+
+        def shift(c, hi, eng):
+            cols = slice(c * P, (c + 1) * P)
+            if hi == 0:
+                e8[c] = fin_pool.tile([P, 8, P], F32, name="e8")
+            rows = slice(4 * hi, 4 * hi + 4)
+            eng.tensor_tensor(out=e8[c][:, rows, :], in0=g8[:, rows, cols], in1=gm[c].unsqueeze(1).to_broadcast([P, 4, P]), op=ALU.subtract)
+
+        def expo(c, hi):
+            rows = slice(4 * hi, 4 * hi + 4)
+            nc.scalar.activation(out=e8[c][:, rows, :], in_=e8[c][:, rows, :], func=ACT.Exp)
 
         def sum_z(c):
-            zt[c] = ps_xt.tile([P, P], F32, name="xt")
+            zt[c] = ps_sum.tile([P, P], F32, name="zt")
             for s in range(8):
                 nc.tensor.matmul(out=zt[c], lhsT=e8[c][:, s, :], rhs=ident, is_transpose=True, start=(s == 0), stop=(s == 7))
 
-        def weigh(c):
+        def weigh_lo(c, eng):
             cols = slice(c * P, (c + 1) * P)
             p8[c] = fin_pool.tile([P, 8, P], F32, name="p8")
-            nc.vector.tensor_tensor(out=p8[c], in0=e8[c], in1=kv8[:, :, cols], op=ALU.mult)
-            at[c] = ps_mx.tile([P, P], F32, name="acc%d" % c)
+            eng.tensor_tensor(out=p8[c][:, 0:4, :], in0=e8[c][:, 0:4, :], in1=kv4[:, :, cols], op=ALU.mult)
+
+        def weigh_hi(c):
+            nc.vector.tensor_tensor(out=p8[c][:, 4:8, :], in0=e8[c][:, 4:8, :], in1=acc[c, 3].rearrange("p (r w) -> p r w", r=RATIO), op=ALU.mult)
+
+        def sum_a(c):
+            at[c] = ps_sum.tile([P, P], F32, name="at")
             for s in range(8):
                 nc.tensor.matmul(out=at[c], lhsT=p8[c][:, s, :], rhs=ident, is_transpose=True, start=(s == 0), stop=(s == 7))
 
@@ -264,90 +267,128 @@ def tile_deepseekv4attention_pa_kernel(tc, hidden_bytes, hidden_scale, wkv, wgat
             nc.vector.tensor_tensor(out=o1[c], in0=at[c], in1=rz[c], op=ALU.mult)
             nc.sync.dma_start(out=o1_view[c], in_=o1[c])
             o0[c] = fin_pool.tile([P, P], F32, name="o0")
-            nc.scalar.copy(out=o0[c][:, 0:64], in_=o1[c][:, 0:64])
 
-        def rot_mul(c):
+        def rot_a(c):
             rot = o1[c][:, 64:128].rearrange("p (j e) -> p j e", e=2)
-            tj = slice(c * HALF, (c + 1) * HALF)
             t1[c] = fin_pool.tile([P, HALF, 2], F32, name="t1")
+            nc.vector.tensor_tensor(out=t1[c], in0=rot, in1=cc[:, c * HALF:(c + 1) * HALF, :], op=ALU.mult)
+
+        def rot_b(c):
+            rot = o1[c][:, 64:128].rearrange("p (j e) -> p j e", e=2)
             t2[c] = fin_pool.tile([P, HALF, 2], F32, name="t2")
-            nc.vector.tensor_tensor(out=t1[c], in0=rot, in1=cc[:, tj, :], op=ALU.mult)
-            nc.vector.tensor_tensor(out=t2[c], in0=rot[:, :, ::-1], in1=ss[:, tj, :], op=ALU.mult)
+            nc.vector.tensor_tensor(out=t2[c], in0=rot[:, :, ::-1], in1=ss[:, c * HALF:(c + 1) * HALF, :], op=ALU.mult)
 
         def rot_add(c):
             nc.vector.tensor_tensor(out=o0[c][:, 64:128].rearrange("p (j e) -> p j e", e=2), in0=t1[c], in1=t2[c], op=ALU.add)
+
+        def plain_half(c):
+            nc.scalar.copy(out=o0[c][:, 0:64], in_=o1[c][:, 0:64])
+
+        def store0(c):
             nc.sync.dma_start(out=o0_view[c], in_=o0[c])
 
-        w_piece = {0: ("gate", 0, 0), 1: ("gate", 0, 1), 3: ("kv", 1, 0), 5: ("kv", 1, 1)}
-        for i in range(RATIO * NCH):
-            widen(i)
-            turn(i)
-            gather(i)
-            if i in w_piece:
-                interleave_w(*w_piece[i])
-            if i == 6:
-                quantize_hidden(0, 0)
-            if i == 8:
-                quantize_w()
-                project(0, 0, GATE, (0, 1))
-            if i == 9:
-                project(0, 0, KV, (0, 1))
-            if i == 10:
-                quantize_hidden(1, 0)
-                project(1, 0, GATE, (0,))
-            if i == 11:
-                project(1, 0, GATE, (1,))
-            if i == 12:
-                project(1, 0, KV, (0,))
-            if i == 13:
-                project(1, 0, KV, (1,))
-            if i == 14:
-                quantize_hidden(2, 0)
-                project(2, 0, GATE, (0,))
-            if i == 15:
-                project(2, 0, GATE, (1,))
-        project(2, 0, KV, (0,))
-        quantize_hidden(3, 0)
-        project(3, 0, GATE, (0, 1))
-        project(2, 0, KV, (1,))
-        project(3, 0, KV, (0, 1))
-        pair_max(gmax, 0)
-        pair_max(hmax, 4)
-        more_max(gmax, 2)
-        more_max(hmax, 6)
-        quantize_hidden(3, 1)
-        join_max()
-        project(3, 1, GATE, (0, 1))
-        run_max(3, 0, 256)
-        run_max(7, 0, 256)
-        shift(0)
-        run_max(3, 256, NW)
-        shift(1)
-        project(3, 1, KV, (0, 1))
-        sum_z(0)
-        run_max(7, 256, NW)
-        weigh(0)
-        sum_z(1)
-        shift(2)
-        weigh(1)
-        shift(3)
+        cast(0)
+        cast(1)
+        cast(2)
+        cast(3)
+        sin_tables()
+        turn(0)
+        for i in range(NT):
+            c, r = divmod(i, RATIO)
+            pc = c - 1
+            sc = c - 2
+            if i + 1 < NT:
+                turn(i + 1)
+            if 4 <= i + LEAD < NT:
+                cast(i + LEAD)
+            mult(i)
+            if i == 4:
+                quantize_w(0)
+            if i == 5:
+                quantize_w(1)
+            if r == 0:
+                if sc >= 0:
+                    shift(sc, 0, nc.gpsimd)
+                    shift(sc, 1, nc.gpsimd)
+                if sc >= 1:
+                    plain_half(sc - 1)
+                    store0(sc - 1)
+                if pc >= 0:
+                    project(pc, 0)
+                    evac_gate(pc, 0)
+            if r == 1:
+                if sc >= 0:
+                    expo(sc, 0)
+                    expo(sc, 1)
+                    weigh_lo(sc, nc.gpsimd)
+                if pc >= 0:
+                    project(pc, 1)
+            if r == 2:
+                if pc >= 0:
+                    evac_gate(pc, 1)
+                    project(pc, 2)
+            if r == 3:
+                if sc >= 0:
+                    sum_z(sc)
+                    weigh_hi(sc)
+                    sum_a(sc)
+                if pc >= 0:
+                    project(pc, 3)
+                    evac_kvlo(pc)
+                quantize_hidden(c)
+                if sc >= 0:
+                    recip(sc)
+                    norm(sc)
+                if pc >= 0:
+                    max1(pc)
+                if sc >= 0:
+                    rot_a(sc)
+                    rot_b(sc)
+                if pc >= 0:
+                    max2(pc)
+                if sc >= 0:
+                    rot_add(sc)
+                if pc >= 0:
+                    max3(pc)
+        shift(2, 0, nc.vector)
+        shift(2, 1, nc.vector)
+        plain_half(1)
+        store0(1)
+        project(3, 0)
+        project(3, 1)
+        project(3, 2)
+        project(3, 3, ps_xt)
+        evac_gate(3, 0)
+        expo(2, 0)
+        evac_gate(3, 1)
+        expo(2, 1)
+        evac_kvlo(3)
         sum_z(2)
-        recip(0)
-        weigh(2)
-        sum_z(3)
-        norm(0)
-        rot_mul(0)
-        recip(1)
-        weigh(3)
-        rot_add(0)
-        norm(1)
+        weigh_lo(2, nc.vector)
+        max1(3)
+        weigh_hi(2)
+        max2(3)
         recip(2)
-        rot_mul(1)
-        recip(3)
+        max3(3)
+        sum_a(2)
+        shift(3, 0, nc.vector)
+        shift(3, 1, nc.vector)
+        expo(3, 0)
+        expo(3, 1)
         norm(2)
-        rot_add(1)
-        rot_mul(2)
-        norm(3)
+        plain_half(2)
+        rot_a(2)
+        rot_b(2)
+        weigh_lo(3, nc.vector)
         rot_add(2)
-        rot_mul(3)
+        store0(2)
+        weigh_hi(3)
+        sum_z(3)
+        sum_a(3)
+        recip(3)
+        norm(3)
+        plain_half(3)
+        rot_a(3)
+        rot_b(3)
         rot_add(3)
+        store0(3)

@@ -27,7 +27,7 @@ THETA = 10000.0
 GW = 520
 TWO_PI = 2.0 * math.pi
 LEAD = 3
-VCAST = (2, 3)
+VCAST = (2,)
 
 
 def tile_deepseekv4attention_pa_kernel(tc, hidden_bytes, hidden_scale, wkv, wgate, ape, out_0, out_1):
@@ -43,8 +43,9 @@ def tile_deepseekv4attention_pa_kernel(tc, hidden_bytes, hidden_scale, wkv, wgat
         grp_pool = ctx.enter_context(tc.tile_pool(name="grp", bufs=2))
         code_pool = ctx.enter_context(tc.tile_pool(name="codes", bufs=2))
         fin_pool = ctx.enter_context(tc.tile_pool(name="fin", bufs=2))
-        ps_xt = ctx.enter_context(tc.psum_pool(name="ps_xt", bufs=2))
-        ps_mx = ctx.enter_context(tc.psum_pool(name="ps_mx", bufs=1))
+        ps_xt = ctx.enter_context(tc.psum_pool(name="ps_xt", bufs=3))
+        ps_ab = ctx.enter_context(tc.psum_pool(name="ps_ab", bufs=2))
+        ps_k = ctx.enter_context(tc.psum_pool(name="ps_k", bufs=1))
         ps_sum = ctx.enter_context(tc.psum_pool(name="ps_sum", bufs=1))
         ctx.enter_context(tc.manual_schedule())
 
@@ -91,26 +92,33 @@ def tile_deepseekv4attention_pa_kernel(tc, hidden_bytes, hidden_scale, wkv, wgat
         nc.gpsimd.memset(kv4[:, :, 0:1], 0.0)
 
         pos = const.tile([P, NCH], F32, name="pos")
-        nc.vector.tensor_copy(out=pos, in_=pos_i)
         coarse = const.tile([P, NCH, 4], F32, name="coarse")
-        for a in range(4):
-            nc.vector.tensor_scalar(out=coarse[:, :, a], in0=pos, scalar1=THETA ** (-8 * a / HALF), scalar2=None, op0=ALU.mult)
         turns = const.tile([P, NCH * 4, 8], F32, name="turns")
-        for b in range(8):
-            nc.vector.tensor_scalar(out=turns[:, :, b], in0=coarse.rearrange("p c a -> p (c a)"), scalar1=THETA ** (-b / HALF) / TWO_PI, scalar2=None, op0=ALU.mult)
         turns_f = turns.rearrange("p q b -> p (q b)")
         whole_i = const.tile([P, NCH * HALF], I32, name="whole_i")
-        nc.vector.tensor_copy(out=whole_i, in_=turns_f)
         whole = const.tile([P, NCH * HALF], F32, name="whole")
-        nc.vector.tensor_copy(out=whole, in_=whole_i)
         frac = const.tile([P, NCH * HALF], F32, name="frac")
-        nc.vector.tensor_tensor(out=frac, in0=turns_f, in1=whole, op=ALU.subtract)
         frac_c = const.tile([P, NCH * HALF], F32, name="frac_c")
-        nc.vector.tensor_scalar(out=frac_c, in0=frac, scalar1=0.25, scalar2=None, op0=ALU.add)
         neg_s = const.tile([P, NCH * HALF], F32, name="neg_s")
-        nc.vector.scalar_tensor_tensor(out=neg_s, in0=frac, scalar=0.5, in1=frac, op0=ALU.is_gt, op1=ALU.subtract)
         neg_c = const.tile([P, NCH * HALF], F32, name="neg_c")
-        nc.vector.scalar_tensor_tensor(out=neg_c, in0=frac_c, scalar=0.5, in1=frac_c, op0=ALU.is_gt, op1=ALU.subtract)
+        nc.vector.tensor_copy(out=pos, in_=pos_i)
+        for a in range(4):
+            nc.vector.tensor_scalar(out=coarse[:, :, a], in0=pos, scalar1=THETA ** (-8 * a / HALF), scalar2=None, op0=ALU.mult)
+        for b in range(8):
+            nc.vector.tensor_scalar(out=turns[:, :, b], in0=coarse.rearrange("p c a -> p (c a)"), scalar1=THETA ** (-b / HALF) / TWO_PI, scalar2=None, op0=ALU.mult)
+        nc.vector.tensor_copy(out=whole_i, in_=turns_f)
+
+        def table_step(k):
+            if k == 0:
+                nc.vector.tensor_copy(out=whole, in_=whole_i)
+            if k == 1:
+                nc.vector.tensor_tensor(out=frac, in0=turns_f, in1=whole, op=ALU.subtract)
+            if k == 2:
+                nc.vector.tensor_scalar(out=frac_c, in0=frac, scalar1=0.25, scalar2=None, op0=ALU.add)
+                nc.vector.scalar_tensor_tensor(out=neg_s, in0=frac, scalar=0.5, in1=frac, op0=ALU.is_gt, op1=ALU.subtract)
+            if k == 3:
+                nc.vector.scalar_tensor_tensor(out=neg_c, in0=frac_c, scalar=0.5, in1=frac_c, op0=ALU.is_gt, op1=ALU.subtract)
+
         cc = const.tile([P, NCH * HALF, 2], F32, name="cc")
         ss = const.tile([P, NCH * HALF, 2], F32, name="ss")
 
@@ -137,9 +145,6 @@ def tile_deepseekv4attention_pa_kernel(tc, hidden_bytes, hidden_scale, wkv, wgat
         for kind in range(2):
             for g in range(2):
                 interleave_w(kind, g)
-        ape_t = const.tile([P, 8], F32, name="ape_t")
-        for h in range(2):
-            nc.gpsimd.tensor_copy(out=ape_t[:, 4 * h:4 * h + 4], in_=ape_b[h])
 
         xb = {}
         xt = {}
@@ -150,7 +155,10 @@ def tile_deepseekv4attention_pa_kernel(tc, hidden_bytes, hidden_scale, wkv, wgat
 
         def cast(i):
             xb[i] = xb_pool.tile([P, HID], BF16, name="xb")
-            if i in VCAST:
+            if i == 0:
+                nc.scalar.copy(out=xb[i][:, 0:512], in_=hb[i][:, 0:512].bitcast(FP8))
+                nc.vector.tensor_copy(out=xb[i][:, 512:1024], in_=hb[i][:, 512:1024].bitcast(FP8))
+            elif i in VCAST:
                 nc.vector.tensor_copy(out=xb[i], in_=hb[i].bitcast(FP8))
             else:
                 nc.scalar.copy(out=xb[i], in_=hb[i].bitcast(FP8))
@@ -167,38 +175,44 @@ def tile_deepseekv4attention_pa_kernel(tc, hidden_bytes, hidden_scale, wkv, wgat
             if r == 0:
                 grp[c] = grp_pool.tile([P, 4 * HID], BF16, name="grp", align_bytes=64)
             nc.vector.tensor_tensor(
-                out=grp[c].rearrange("p (g r x) -> p g r x", g=2, r=RATIO)[:, :, r, :].rearrange("p g (w u e) -> p g w u e", u=2, e=2),
+                out=grp[c].rearrange("p (h g r x) -> p h g r x", h=2, g=2, r=2)[:, r // 2, :, r % 2, :].rearrange("p g (w u e) -> p g w u e", u=2, e=2),
                 in0=xt[i].rearrange("p u g w -> p (u g w)").bitcast(BF16).rearrange("p (u g w e) -> p g w u e", u=2, g=2, e=2),
                 in1=scale_col.rearrange("p g (u e) -> p g u e", e=2).unsqueeze(2).to_broadcast([P, 2, P, 2, 2]),
                 op=ALU.mult,
             )
 
-        def quantize_hidden(c):
-            hcodes[c] = code_pool.tile([P, 1024], U32, name="hcodes", align_bytes=64)
-            hscales[c] = code_pool.tile([P, 1024], U8, name="hscales", align_bytes=64)
-            nc.vector.quantize_mx(out=hcodes[c].bitcast(FP8X4), scales=hscales[c], in_=grp[c])
+        def quantize_hidden(c, h):
+            if h == 0:
+                hcodes[c] = code_pool.tile([P, 1024], U32, name="hcodes", align_bytes=64)
+                hscales[c] = code_pool.tile([P, 1024], U8, name="hscales", align_bytes=64)
+            cols = slice(512 * h, 512 * (h + 1))
+            nc.vector.quantize_mx(out=hcodes[c][:, cols].bitcast(FP8X4), scales=hscales[c][:, cols], in_=grp[c][:, 2048 * h:2048 * (h + 1)])
 
-        def project(c, m, pool=None):
+        def project(c, m, halves=(0, 1), pool=None):
             kind, hi = divmod(m, 2)
-            if pool is None:
-                acc[c, m] = ps_mx.tile([P, NW], F32, name="acc%d" % m)
-            else:
-                acc[c, m] = pool.tile([P, NW], F32, name="xt")
-            for g in range(2):
-                wc = slice(512 * kind + 256 * g + P * hi, 512 * kind + 256 * g + P * (hi + 1))
-                hc = slice(512 * g, 512 * (g + 1))
-                nc.tensor.matmul_mx(
-                    out=acc[c, m],
-                    lhsT=wcodes[:, wc].bitcast(FP8X4), lhsT_scale=wscales[:, wc],
-                    rhs=hcodes[c][:, hc].bitcast(FP8X4), rhs_scale=hscales[c][:, hc],
-                    start=(g == 0), stop=(g == 1),
-                )
+            if halves[0] == 0:
+                if pool is not None:
+                    acc[c, m] = pool.tile([P, NW], F32, name="xt")
+                elif m == 3:
+                    acc[c, m] = ps_k.tile([P, NW], F32, name="kvhi")
+                else:
+                    acc[c, m] = ps_ab.tile([P, NW], F32, name="ab")
+            for h in halves:
+                for g in range(2):
+                    wc = slice(512 * kind + 256 * g + P * hi, 512 * kind + 256 * g + P * (hi + 1))
+                    hc = slice(512 * h + 256 * g, 512 * h + 256 * (g + 1))
+                    nc.tensor.matmul_mx(
+                        out=acc[c, m][:, 256 * h:256 * (h + 1)],
+                        lhsT=wcodes[:, wc].bitcast(FP8X4), lhsT_scale=wscales[:, wc],
+                        rhs=hcodes[c][:, hc].bitcast(FP8X4), rhs_scale=hscales[c][:, hc],
+                        start=(g == 0), stop=(g == 1),
+                    )
 
-        def evac_gate(c, hi):
-            for r in range(RATIO):
+        def evac_gate(c, hi, slots=(0, 1, 2, 3)):
+            for r in slots:
                 s = 4 * hi + r
                 cols = slice(1 - hi + c * P, 1 - hi + (c + 1) * P)
-                nc.scalar.activation(out=g8[:, s, cols], in_=acc[c, hi][:, r * P:(r + 1) * P], func=ACT.Identity, bias=ape_t[:, s:s + 1], scale=1.0)
+                nc.scalar.activation(out=g8[:, s, cols], in_=acc[c, hi][:, r * P:(r + 1) * P], func=ACT.Identity, bias=ape_b[hi][:, r:r + 1], scale=1.0)
 
         def evac_kvlo(c):
             nc.scalar.copy(out=kv4[:, :, 1 + c * P:1 + (c + 1) * P], in_=acc[c, 2].rearrange("p (r w) -> p r w", r=RATIO))
@@ -215,6 +229,8 @@ def tile_deepseekv4attention_pa_kernel(tc, hidden_bytes, hidden_scale, wkv, wgat
         o0 = {}
         t1 = {}
         t2 = {}
+        crz = {}
+        srz = {}
 
         def max1(c):
             cols = slice(c * P, (c + 1) * P)
@@ -229,6 +245,15 @@ def tile_deepseekv4attention_pa_kernel(tc, hidden_bytes, hidden_scale, wkv, wgat
             gm[c] = fin_pool.tile([P, P], F32, name="gm")
             nc.vector.tensor_tensor(out=gm[c], in0=m2[c][:, 0, :], in1=m2[c][:, 1, :], op=ALU.max)
 
+        def max_pair(c, h):
+            cols = slice(c * P, (c + 1) * P)
+            m4[c, h] = fin_pool.tile([P, 2, P], F32, name="mp%d" % h)
+            nc.vector.tensor_tensor(out=m4[c, h], in0=g8[:, 2 * h:2 * h + 2, cols], in1=g8[:, 4 + 2 * h:6 + 2 * h, cols], op=ALU.max)
+
+        def max_join(c):
+            m2[c] = fin_pool.tile([P, 2, P], F32, name="m2")
+            nc.vector.tensor_tensor(out=m2[c], in0=m4[c, 0], in1=m4[c, 1], op=ALU.max)
+
         def shift(c, hi, eng):
             cols = slice(c * P, (c + 1) * P)
             if hi == 0:
@@ -241,7 +266,7 @@ def tile_deepseekv4attention_pa_kernel(tc, hidden_bytes, hidden_scale, wkv, wgat
             nc.scalar.activation(out=e8[c][:, rows, :], in_=e8[c][:, rows, :], func=ACT.Exp)
 
         def sum_z(c):
-            zt[c] = ps_sum.tile([P, P], F32, name="zt")
+            zt[c] = ps_sum.tile([P, P], F32, name="zt") if c < 3 else ps_xt.tile([P, P], F32, name="xt")
             for s in range(8):
                 nc.tensor.matmul(out=zt[c], lhsT=e8[c][:, s, :], rhs=ident, is_transpose=True, start=(s == 0), stop=(s == 7))
 
@@ -254,7 +279,7 @@ def tile_deepseekv4attention_pa_kernel(tc, hidden_bytes, hidden_scale, wkv, wgat
             nc.vector.tensor_tensor(out=p8[c][:, 4:8, :], in0=e8[c][:, 4:8, :], in1=acc[c, 3].rearrange("p (r w) -> p r w", r=RATIO), op=ALU.mult)
 
         def sum_a(c):
-            at[c] = ps_sum.tile([P, P], F32, name="at")
+            at[c] = ps_sum.tile([P, P], F32, name="at") if c < 3 else ps_ab.tile([P, P], F32, name="ab")
             for s in range(8):
                 nc.tensor.matmul(out=at[c], lhsT=p8[c][:, s, :], rhs=ident, is_transpose=True, start=(s == 0), stop=(s == 7))
 
@@ -281,114 +306,170 @@ def tile_deepseekv4attention_pa_kernel(tc, hidden_bytes, hidden_scale, wkv, wgat
         def rot_add(c):
             nc.vector.tensor_tensor(out=o0[c][:, 64:128].rearrange("p (j e) -> p j e", e=2), in0=t1[c], in1=t2[c], op=ALU.add)
 
+        def fold_tables(c):
+            rzr = rz[c][:, 64:128].rearrange("p (j e) -> p j e", e=2)
+            tj = slice(c * HALF, (c + 1) * HALF)
+            crz[c] = fin_pool.tile([P, HALF, 2], F32, name="crz")
+            srz[c] = fin_pool.tile([P, HALF, 2], F32, name="srz")
+            nc.vector.tensor_tensor(out=crz[c], in0=rzr, in1=cc[:, tj, :], op=ALU.mult)
+            nc.vector.tensor_tensor(out=srz[c], in0=rzr[:, :, ::-1], in1=ss[:, tj, :], op=ALU.mult)
+
+        def rot_folded(c):
+            atr = at[c][:, 64:128].rearrange("p (j e) -> p j e", e=2)
+            t1[c] = fin_pool.tile([P, HALF, 2], F32, name="t1")
+            t2[c] = fin_pool.tile([P, HALF, 2], F32, name="t2")
+            nc.vector.tensor_tensor(out=t1[c], in0=atr, in1=crz[c], op=ALU.mult)
+            nc.vector.tensor_tensor(out=t2[c], in0=atr[:, :, ::-1], in1=srz[c], op=ALU.mult)
+
         def plain_half(c):
             nc.scalar.copy(out=o0[c][:, 0:64], in_=o1[c][:, 0:64])
 
         def store0(c):
             nc.sync.dma_start(out=o0_view[c], in_=o0[c])
 
+        table_step(0)
+        table_step(1)
         cast(0)
+        table_step(2)
         cast(1)
         cast(2)
-        cast(3)
-        sin_tables()
+        table_step(3)
         turn(0)
         for i in range(NT):
             c, r = divmod(i, RATIO)
             pc = c - 1
             sc = c - 2
-            if i + 1 < NT:
+            if i + 1 < NT and (r != 3 or c == 0):
                 turn(i + 1)
-            if 4 <= i + LEAD < NT:
-                cast(i + LEAD)
-            mult(i)
-            if i == 4:
-                quantize_w(0)
-            if i == 5:
-                quantize_w(1)
             if r == 0:
                 if sc >= 0:
                     shift(sc, 0, nc.gpsimd)
                     shift(sc, 1, nc.gpsimd)
-                if sc >= 1:
-                    plain_half(sc - 1)
-                    store0(sc - 1)
-                if pc >= 0:
+                if pc >= 1:
                     project(pc, 0)
                     evac_gate(pc, 0)
+                if sc >= 1:
+                    plain_half(sc - 1)
             if r == 1:
                 if sc >= 0:
                     expo(sc, 0)
-                    expo(sc, 1)
                     weigh_lo(sc, nc.gpsimd)
-                if pc >= 0:
+                if pc >= 1:
                     project(pc, 1)
-            if r == 2:
-                if pc >= 0:
                     evac_gate(pc, 1)
+                if sc >= 0:
+                    expo(sc, 1)
+            if r == 2:
+                if i == 6:
+                    project(0, 0)
+                    evac_gate(0, 0)
+                    project(0, 1)
+                    evac_gate(0, 1)
+                if pc >= 1:
                     project(pc, 2)
+                    evac_kvlo(pc)
             if r == 3:
+                if i == 7:
+                    project(0, 2)
+                    evac_kvlo(0)
                 if sc >= 0:
                     sum_z(sc)
-                    weigh_hi(sc)
-                    sum_a(sc)
-                if pc >= 0:
-                    project(pc, 3)
-                    evac_kvlo(pc)
-                quantize_hidden(c)
-                if sc >= 0:
-                    recip(sc)
-                    norm(sc)
+            if 3 <= i + LEAD < NT:
+                cast(i + LEAD)
+            if i == 3:
+                sin_tables()
+            mult(i)
+            if i == 5:
+                quantize_hidden(0, 0)
+                quantize_hidden(0, 1)
+                quantize_w(0)
+                quantize_w(1)
+            if r == 3 and c < 3:
                 if pc >= 0:
                     max1(pc)
+                if sc >= 0:
+                    weigh_hi(sc)
+                    sum_a(sc)
+                    recip(sc)
+                if pc >= 0:
+                    project(pc, 3)
+                if c > 0:
+                    turn(i + 1)
+                if sc >= 1:
+                    rot_add(sc - 1)
+                    store0(sc - 1)
+                if c > 0:
+                    quantize_hidden(c, 0)
+                if pc >= 0:
+                    max2(pc)
+                if sc >= 0:
+                    norm(sc)
+                if c > 0:
+                    quantize_hidden(c, 1)
                 if sc >= 0:
                     rot_a(sc)
                     rot_b(sc)
                 if pc >= 0:
-                    max2(pc)
-                if sc >= 0:
-                    rot_add(sc)
-                if pc >= 0:
                     max3(pc)
-        shift(2, 0, nc.vector)
-        shift(2, 1, nc.vector)
+        max1(2)
+        quantize_hidden(3, 0)
+        project(3, 0, (0,))
+        project(3, 1, (0,))
+        evac_gate(3, 0, (0, 1))
+        evac_gate(3, 1, (0, 1))
+        quantize_hidden(3, 1)
+        project(3, 0, (1,))
+        project(3, 1, (1,))
+        evac_gate(3, 0, (2, 3))
+        evac_gate(3, 1, (2, 3))
+        weigh_hi(1)
+        sum_a(1)
+        project(2, 3)
+        project(3, 2, (0, 1), ps_xt)
+        project(3, 3, (0, 1), ps_xt)
+        max2(2)
+        recip(1)
+        max_pair(3, 0)
+        rot_add(0)
+        store0(0)
+        max3(2)
+        norm(1)
         plain_half(1)
-        store0(1)
-        project(3, 0)
-        project(3, 1)
-        project(3, 2)
-        project(3, 3, ps_xt)
-        evac_gate(3, 0)
+        max_pair(3, 1)
+        shift(2, 0, nc.vector)
         expo(2, 0)
-        evac_gate(3, 1)
+        max_join(3)
+        shift(2, 1, nc.vector)
         expo(2, 1)
         evac_kvlo(3)
         sum_z(2)
-        weigh_lo(2, nc.vector)
-        max1(3)
-        weigh_hi(2)
-        max2(3)
-        recip(2)
         max3(3)
-        sum_a(2)
+        rot_a(1)
+        rot_b(1)
+        weigh_lo(2, nc.vector)
         shift(3, 0, nc.vector)
-        shift(3, 1, nc.vector)
         expo(3, 0)
+        shift(3, 1, nc.vector)
         expo(3, 1)
+        weigh_hi(2)
+        sum_a(2)
+        sum_z(3)
+        rot_add(1)
+        store0(1)
+        recip(2)
+        weigh_lo(3, nc.vector)
+        weigh_hi(3)
+        sum_a(3)
         norm(2)
         plain_half(2)
+        recip(3)
         rot_a(2)
         rot_b(2)
-        weigh_lo(3, nc.vector)
+        fold_tables(3)
         rot_add(2)
         store0(2)
-        weigh_hi(3)
-        sum_z(3)
-        sum_a(3)
-        recip(3)
+        rot_folded(3)
         norm(3)
         plain_half(3)
-        rot_a(3)
-        rot_b(3)
         rot_add(3)
         store0(3)

@@ -27,7 +27,7 @@ THETA = 10000.0
 GW = 520
 TWO_PI = 2.0 * math.pi
 LEAD = 3
-VCAST = (2,)
+VCAST = (1,)
 
 
 def tile_deepseekv4attention_pa_kernel(tc, hidden_bytes, hidden_scale, wkv, wgate, ape, out_0, out_1):
@@ -50,7 +50,6 @@ def tile_deepseekv4attention_pa_kernel(tc, hidden_bytes, hidden_scale, wkv, wgat
         ctx.enter_context(tc.manual_schedule())
 
         scale_col = const.tile([P, 2, 4], F32, name="scale_col")
-        nc.sync.dma_start(out=scale_col, in_=hidden_scale.rearrange("a b (g p t) -> (a b p) g t", g=2, t=4))
         hb = {}
 
         def load_bytes(i):
@@ -65,11 +64,15 @@ def tile_deepseekv4attention_pa_kernel(tc, hidden_bytes, hidden_scale, wkv, wgat
             nc.sync.dma_start(out=t, in_=w.rearrange("(g p j) n -> p g j n", g=2, p=P, j=4))
             wraw[key] = t
 
-        for i in range(4):
-            load_bytes(i)
+        load_bytes(0)
+        nc.sync.dma_start(out=scale_col, in_=hidden_scale.rearrange("a b (g p t) -> (a b p) g t", g=2, t=4))
+        load_bytes(1)
+        load_bytes(2)
         load_w("gate", wgate)
+        load_bytes(3)
+        load_bytes(4)
         load_w("kv", wkv)
-        for i in range(4, 8):
+        for i in range(5, 8):
             load_bytes(i)
         ape_b = []
         with nc.allow_non_contiguous_dma(reason="ape: 1024 values, one feature to a partition"):
@@ -80,8 +83,8 @@ def tile_deepseekv4attention_pa_kernel(tc, hidden_bytes, hidden_scale, wkv, wgat
         for i in range(8, NT):
             load_bytes(i)
 
-        pos_i = const.tile([P, NCH], I32, name="pos_i")
-        nc.gpsimd.iota(pos_i, pattern=[[RATIO * P, NCH]], base=0, channel_multiplier=RATIO)
+        pos = const.tile([P, NCH], F32, name="pos")
+        nc.gpsimd.iota(pos, pattern=[[RATIO * P, NCH]], base=0, channel_multiplier=RATIO, allow_small_or_imprecise_dtypes=True)
         ident = const.tile([P, P], F32, name="ident")
         make_identity(nc, ident)
         first = const.tile([P, 2], F32, name="first")
@@ -91,7 +94,6 @@ def tile_deepseekv4attention_pa_kernel(tc, hidden_bytes, hidden_scale, wkv, wgat
         nc.gpsimd.memset(g8[:, 0:4, 0:1], -1.0e30)
         nc.gpsimd.memset(kv4[:, :, 0:1], 0.0)
 
-        pos = const.tile([P, NCH], F32, name="pos")
         coarse = const.tile([P, NCH, 4], F32, name="coarse")
         turns = const.tile([P, NCH * 4, 8], F32, name="turns")
         turns_f = turns.rearrange("p q b -> p (q b)")
@@ -101,7 +103,6 @@ def tile_deepseekv4attention_pa_kernel(tc, hidden_bytes, hidden_scale, wkv, wgat
         frac_c = const.tile([P, NCH * HALF], F32, name="frac_c")
         neg_s = const.tile([P, NCH * HALF], F32, name="neg_s")
         neg_c = const.tile([P, NCH * HALF], F32, name="neg_c")
-        nc.vector.tensor_copy(out=pos, in_=pos_i)
         for a in range(4):
             nc.vector.tensor_scalar(out=coarse[:, :, a], in0=pos, scalar1=THETA ** (-8 * a / HALF), scalar2=None, op0=ALU.mult)
         for b in range(8):
@@ -385,13 +386,12 @@ def tile_deepseekv4attention_pa_kernel(tc, hidden_bytes, hidden_scale, wkv, wgat
                 quantize_w(0)
                 quantize_w(1)
             if r == 3 and c < 3:
-                if pc >= 0:
-                    max1(pc)
                 if sc >= 0:
                     weigh_hi(sc)
                     sum_a(sc)
                     recip(sc)
                 if pc >= 0:
+                    max1(pc)
                     project(pc, 3)
                 if c > 0:
                     turn(i + 1)
@@ -411,7 +411,9 @@ def tile_deepseekv4attention_pa_kernel(tc, hidden_bytes, hidden_scale, wkv, wgat
                     rot_b(sc)
                 if pc >= 0:
                     max3(pc)
-        max1(2)
+        weigh_hi(1)
+        sum_a(1)
+        project(2, 3)
         quantize_hidden(3, 0)
         project(3, 0, (0,))
         project(3, 1, (0,))
@@ -422,54 +424,52 @@ def tile_deepseekv4attention_pa_kernel(tc, hidden_bytes, hidden_scale, wkv, wgat
         project(3, 1, (1,))
         evac_gate(3, 0, (2, 3))
         evac_gate(3, 1, (2, 3))
-        weigh_hi(1)
-        sum_a(1)
-        project(2, 3)
         project(3, 2, (0, 1), ps_xt)
         project(3, 3, (0, 1), ps_xt)
-        max2(2)
+        max1(2)
         recip(1)
         max_pair(3, 0)
+        max2(2)
         rot_add(0)
         store0(0)
-        max3(2)
         norm(1)
         plain_half(1)
         max_pair(3, 1)
+        max3(2)
+        rot_a(1)
+        rot_b(1)
+        max_join(3)
         shift(2, 0, nc.vector)
         expo(2, 0)
-        max_join(3)
+        max3(3)
         shift(2, 1, nc.vector)
         expo(2, 1)
         evac_kvlo(3)
         sum_z(2)
-        max3(3)
-        rot_a(1)
-        rot_b(1)
-        weigh_lo(2, nc.vector)
         shift(3, 0, nc.vector)
         expo(3, 0)
+        weigh_lo(2, nc.vector)
         shift(3, 1, nc.vector)
         expo(3, 1)
+        sum_z(3)
         weigh_hi(2)
         sum_a(2)
-        sum_z(3)
         rot_add(1)
         store0(1)
         recip(2)
         weigh_lo(3, nc.vector)
+        recip(3)
         weigh_hi(3)
         sum_a(3)
         norm(2)
         plain_half(2)
-        recip(3)
+        fold_tables(3)
         rot_a(2)
         rot_b(2)
-        fold_tables(3)
-        rot_add(2)
-        store0(2)
         rot_folded(3)
         norm(3)
         plain_half(3)
+        rot_add(2)
+        store0(2)
         rot_add(3)
         store0(3)

@@ -166,19 +166,19 @@ def tile_deepseekv4attention_pa_kernel(tc, hidden_bytes, hidden_scale, wkv, wgat
 
         def turn(i):
             words = xb[i].bitcast(F32)
-            xt[i] = ps_xt.tile([P, 2, 2, P], F32, name="xt")
+            xt[i] = ps_xt.tile([P, 2, P, 2], F32, name="xt")
             for g in range(2):
                 for u in range(2):
-                    nc.tensor.transpose(xt[i][:, u, g, :], words[:, 256 * g + u:256 * (g + 1):2], ident)
+                    nc.tensor.transpose(xt[i][:, g, :, u], words[:, 256 * g + u:256 * (g + 1):2], ident)
 
         def mult(i):
             c, r = divmod(i, RATIO)
             if r == 0:
                 grp[c] = grp_pool.tile([P, 4 * HID], BF16, name="grp", align_bytes=64)
             nc.vector.tensor_tensor(
-                out=grp[c].rearrange("p (h g r x) -> p h g r x", h=2, g=2, r=2)[:, r // 2, :, r % 2, :].rearrange("p g (w u e) -> p g w u e", u=2, e=2),
-                in0=xt[i].rearrange("p u g w -> p (u g w)").bitcast(BF16).rearrange("p (u g w e) -> p g w u e", u=2, g=2, e=2),
-                in1=scale_col.rearrange("p g (u e) -> p g u e", e=2).unsqueeze(2).to_broadcast([P, 2, P, 2, 2]),
+                out=grp[c].rearrange("p (h g r x) -> p h g r x", h=2, g=2, r=2)[:, r // 2, :, r % 2, :].rearrange("p g (w t) -> p g w t", t=4),
+                in0=xt[i].rearrange("p g w u -> p (g w u)").bitcast(BF16).rearrange("p (g w t) -> p g w t", g=2, t=4),
+                in1=scale_col.unsqueeze(2).to_broadcast([P, 2, P, 4]),
                 op=ALU.mult,
             )
 

@@ -328,6 +328,14 @@ def tile_deepseekv4attention_pa_kernel(tc, hidden_bytes, hidden_scale, wkv, wgat
         def store0(c):
             nc.sync.dma_start(out=o0_view[c], in_=o0[c])
 
+        idle_ps = {}
+
+        def idle(n):
+            for k in range(n):
+                nc.tensor.matmul(out=idle_ps[0], lhsT=ident, rhs=ident, start=True, stop=True)
+
+        idle_ps[0] = ps_sum.tile([P, P], F32, name="zt")
+        idle(4)
         table_step(0)
         table_step(1)
         cast(0)
@@ -446,12 +454,15 @@ def tile_deepseekv4attention_pa_kernel(tc, hidden_bytes, hidden_scale, wkv, wgat
         expo(2, 1)
         evac_kvlo(3)
         sum_z(2)
+        idle_ps[0] = ps_ab.tile([P, P], F32, name="ab")
+        idle(3)
         shift(3, 0, nc.vector)
         expo(3, 0)
         weigh_lo(2, nc.vector)
         shift(3, 1, nc.vector)
         expo(3, 1)
         sum_z(3)
+        idle(2)
         weigh_hi(2)
         sum_a(2)
         rot_add(1)

@@ -26,7 +26,8 @@ HALF = 32
 THETA = 10000.0
 GW = 520
 TWO_PI = 2.0 * math.pi
-LEAD = 3
+SPATH = (8, 12)
+LEAD = 4
 VCAST = (1,)
 
 
@@ -39,7 +40,7 @@ def tile_deepseekv4attention_pa_kernel(tc, hidden_bytes, hidden_scale, wkv, wgat
     with ExitStack() as ctx:
         const = ctx.enter_context(tc.tile_pool(name="const", bufs=1))
         bytes_pool = ctx.enter_context(tc.tile_pool(name="bytes", bufs=1))
-        xb_pool = ctx.enter_context(tc.tile_pool(name="xb", bufs=5))
+        xb_pool = ctx.enter_context(tc.tile_pool(name="xb", bufs=6))
         grp_pool = ctx.enter_context(tc.tile_pool(name="grp", bufs=2))
         code_pool = ctx.enter_context(tc.tile_pool(name="codes", bufs=2))
         fin_pool = ctx.enter_context(tc.tile_pool(name="fin", bufs=2))
@@ -148,6 +149,7 @@ def tile_deepseekv4attention_pa_kernel(tc, hidden_bytes, hidden_scale, wkv, wgat
                 interleave_w(kind, g)
 
         xb = {}
+        planes = {}
         xt = {}
         grp = {}
         hcodes = {}
@@ -173,8 +175,6 @@ def tile_deepseekv4attention_pa_kernel(tc, hidden_bytes, hidden_scale, wkv, wgat
 
         def mult(i):
             c, r = divmod(i, RATIO)
-            if r == 0:
-                grp[c] = grp_pool.tile([P, 4 * HID], BF16, name="grp", align_bytes=64)
             nc.vector.tensor_tensor(
                 out=grp[c].rearrange("p (h g r x) -> p h g r x", h=2, g=2, r=2)[:, r // 2, :, r % 2, :].rearrange("p g (w t) -> p g w t", t=4),
                 in0=xt[i].rearrange("p g w u -> p (g w u)").bitcast(BF16).rearrange("p (g w t) -> p g w t", g=2, t=4),
@@ -182,8 +182,22 @@ def tile_deepseekv4attention_pa_kernel(tc, hidden_bytes, hidden_scale, wkv, wgat
                 op=ALU.mult,
             )
 
+        def spath_a(i, g):
+            if g == 0:
+                planes[i] = fin_pool.tile([P, 2, 4, P], BF16, name="planes")
+            xv = xt[i].rearrange("p g w u -> p (g w u)").bitcast(BF16).rearrange("p (g w t) -> p g t w", g=2, t=4)
+            for t in range(4):
+                nc.scalar.activation(out=planes[i][:, g, t, :], in_=xv[:, g, t, :], func=ACT.Copy, scale=scale_col[:, g, t:t + 1])
+
+        def spath_b(i):
+            c, r = divmod(i, RATIO)
+            nc.scalar.copy(
+                out=grp[c].rearrange("p (h g r x) -> p h g r x", h=2, g=2, r=2)[:, r // 2, :, r % 2, :].rearrange("p g (w t) -> p g w t", t=4),
+                in_=planes[i].rearrange("p g t w -> p g w t"),
+            )
+
         def quantize_hidden(c, h):
-            if h == 0:
+            if c not in hcodes:
                 hcodes[c] = code_pool.tile([P, 1024], U32, name="hcodes", align_bytes=64)
                 hscales[c] = code_pool.tile([P, 1024], U8, name="hscales", align_bytes=64)
             cols = slice(512 * h, 512 * (h + 1))
@@ -191,7 +205,7 @@ def tile_deepseekv4attention_pa_kernel(tc, hidden_bytes, hidden_scale, wkv, wgat
 
         def project(c, m, halves=(0, 1), pool=None):
             kind, hi = divmod(m, 2)
-            if halves[0] == 0:
+            if (c, m) not in acc:
                 if pool is not None:
                     acc[c, m] = pool.tile([P, NW], F32, name="xt")
                 elif m == 3:
@@ -342,14 +356,19 @@ def tile_deepseekv4attention_pa_kernel(tc, hidden_bytes, hidden_scale, wkv, wgat
         table_step(2)
         cast(1)
         cast(2)
+        cast(3)
         table_step(3)
         turn(0)
+        turned = {0}
         for i in range(NT):
             c, r = divmod(i, RATIO)
             pc = c - 1
             sc = c - 2
-            if i + 1 < NT and (r != 3 or c == 0):
+            if r == 0:
+                grp[c] = grp_pool.tile([P, 4 * HID], BF16, name="grp", align_bytes=64)
+            if i + 1 < NT and (r != 3 or c == 0) and i + 1 not in turned:
                 turn(i + 1)
+                turned.add(i + 1)
             if r == 0:
                 if sc >= 0:
                     shift(sc, 0, nc.gpsimd)
@@ -383,11 +402,14 @@ def tile_deepseekv4attention_pa_kernel(tc, hidden_bytes, hidden_scale, wkv, wgat
                     evac_kvlo(0)
                 if sc >= 0:
                     sum_z(sc)
-            if 3 <= i + LEAD < NT:
+            if LEAD <= i + LEAD < NT:
                 cast(i + LEAD)
+            if i - 1 in SPATH:
+                spath_b(i - 1)
             if i == 3:
                 sin_tables()
-            mult(i)
+            if i not in SPATH:
+                mult(i)
             if i == 5:
                 quantize_hidden(0, 0)
                 quantize_hidden(0, 1)
@@ -401,19 +423,25 @@ def tile_deepseekv4attention_pa_kernel(tc, hidden_bytes, hidden_scale, wkv, wgat
                 if pc >= 0:
                     max1(pc)
                     project(pc, 3)
-                if c > 0:
+                if i + 1 not in turned:
                     turn(i + 1)
+                    turned.add(i + 1)
+                if i + 1 in SPATH:
+                    spath_a(i + 1, 0)
+                    spath_a(i + 1, 1)
+                    turn(i + 2)
+                    turned.add(i + 2)
                 if sc >= 1:
                     rot_add(sc - 1)
                     store0(sc - 1)
                 if c > 0:
-                    quantize_hidden(c, 0)
+                    quantize_hidden(c, 1)
                 if pc >= 0:
                     max2(pc)
                 if sc >= 0:
                     norm(sc)
                 if c > 0:
-                    quantize_hidden(c, 1)
+                    quantize_hidden(c, 0)
                 if sc >= 0:
                     rot_a(sc)
                     rot_b(sc)
@@ -422,27 +450,27 @@ def tile_deepseekv4attention_pa_kernel(tc, hidden_bytes, hidden_scale, wkv, wgat
         weigh_hi(1)
         sum_a(1)
         project(2, 3)
-        quantize_hidden(3, 0)
-        project(3, 0, (0,))
-        project(3, 1, (0,))
-        evac_gate(3, 0, (0, 1))
-        evac_gate(3, 1, (0, 1))
         quantize_hidden(3, 1)
         project(3, 0, (1,))
         project(3, 1, (1,))
         evac_gate(3, 0, (2, 3))
         evac_gate(3, 1, (2, 3))
+        quantize_hidden(3, 0)
+        project(3, 0, (0,))
+        project(3, 1, (0,))
+        evac_gate(3, 0, (0, 1))
+        evac_gate(3, 1, (0, 1))
         project(3, 2, (0, 1), ps_xt)
         project(3, 3, (0, 1), ps_xt)
         max1(2)
         recip(1)
-        max_pair(3, 0)
+        max_pair(3, 1)
         max2(2)
         rot_add(0)
         store0(0)
         norm(1)
         plain_half(1)
-        max_pair(3, 1)
+        max_pair(3, 0)
         max3(2)
         rot_a(1)
         rot_b(1)

@@ -26,7 +26,7 @@ HALF = 32
 THETA = 10000.0
 GW = 520
 TWO_PI = 2.0 * math.pi
-SPATH = (8, 12)
+SPATH = (12,)
 LEAD = 4
 VCAST = (1,)
 

@@ -280,8 +280,15 @@ def tile_deepseekv4attention_pa_kernel(tc, hidden_bytes, hidden_scale, wkv, wgat
             rows = slice(4 * hi, 4 * hi + 4)
             nc.scalar.activation(out=e8[c][:, rows, :], in_=e8[c][:, rows, :], func=ACT.Exp)
 
+        pair = {}
+
         def sum_z(c):
-            zt[c] = ps_sum.tile([P, P], F32, name="zt") if c < 3 else ps_xt.tile([P, P], F32, name="xt")
+            if c == 0:
+                pair["z"] = ps_sum.tile([P, 2, P], F32, name="zt")
+            if c < 2:
+                zt[c] = pair["z"][:, c, :]
+            else:
+                zt[c] = ps_sum.tile([P, P], F32, name="zt") if c < 3 else ps_xt.tile([P, P], F32, name="xt")
             for s in range(8):
                 nc.tensor.matmul(out=zt[c], lhsT=e8[c][:, s, :], rhs=ident, is_transpose=True, start=(s == 0), stop=(s == 7))
 
@@ -294,7 +301,12 @@ def tile_deepseekv4attention_pa_kernel(tc, hidden_bytes, hidden_scale, wkv, wgat
             nc.vector.tensor_tensor(out=p8[c][:, 4:8, :], in0=e8[c][:, 4:8, :], in1=acc[c, 3].rearrange("p (r w) -> p r w", r=RATIO), op=ALU.mult)
 
         def sum_a(c):
-            at[c] = ps_sum.tile([P, P], F32, name="at") if c < 3 else ps_ab.tile([P, P], F32, name="ab")
+            if c == 0:
+                pair["a"] = ps_sum.tile([P, 2, P], F32, name="at")
+            if c < 2:
+                at[c] = pair["a"][:, c, :]
+            else:
+                at[c] = ps_sum.tile([P, P], F32, name="at") if c < 3 else ps_ab.tile([P, P], F32, name="ab")
             for s in range(8):
                 nc.tensor.matmul(out=at[c], lhsT=p8[c][:, s, :], rhs=ident, is_transpose=True, start=(s == 0), stop=(s == 7))
 
@@ -336,6 +348,35 @@ def tile_deepseekv4attention_pa_kernel(tc, hidden_bytes, hidden_scale, wkv, wgat
             nc.vector.tensor_tensor(out=t1[c], in0=atr, in1=crz[c], op=ALU.mult)
             nc.vector.tensor_tensor(out=t2[c], in0=atr[:, :, ::-1], in1=srz[c], op=ALU.mult)
 
+        def recip01():
+            pair["rz"] = fin_pool.tile([P, 2, P], F32, name="rz01")
+            nc.vector.reciprocal(out=pair["rz"], in_=pair["z"])
+
+        def norm01():
+            pair["o1"] = fin_pool.tile([P, 2, P], F32, name="o1p")
+            nc.vector.tensor_tensor(out=pair["o1"], in0=pair["a"], in1=pair["rz"], op=ALU.mult)
+            nc.sync.dma_start(out=o1_view[0:2].rearrange("c p f -> p c f"), in_=pair["o1"])
+            pair["o0"] = fin_pool.tile([P, 2, P], F32, name="o0p")
+
+        def rot_a01():
+            rot = pair["o1"][:, :, 64:128].rearrange("p c (j e) -> p c j e", e=2)
+            pair["t1"] = fin_pool.tile([P, 2, HALF, 2], F32, name="t1p")
+            nc.vector.tensor_tensor(out=pair["t1"], in0=rot, in1=cc[:, 0:2 * HALF, :].rearrange("p (c j) e -> p c j e", c=2), op=ALU.mult)
+
+        def rot_b01():
+            rot = pair["o1"][:, :, 64:128].rearrange("p c (j e) -> p c j e", e=2)
+            pair["t2"] = fin_pool.tile([P, 2, HALF, 2], F32, name="t2p")
+            nc.vector.tensor_tensor(out=pair["t2"], in0=rot[:, :, :, ::-1], in1=ss[:, 0:2 * HALF, :].rearrange("p (c j) e -> p c j e", c=2), op=ALU.mult)
+
+        def rot_add01():
+            nc.vector.tensor_tensor(out=pair["o0"][:, :, 64:128].rearrange("p c (j e) -> p c j e", e=2), in0=pair["t1"], in1=pair["t2"], op=ALU.add)
+
+        def plain01():
+            nc.scalar.copy(out=pair["o0"][:, :, 0:64], in_=pair["o1"][:, :, 0:64])
+
+        def store01():
+            nc.sync.dma_start(out=o0_view[0:2].rearrange("c p f -> p c f"), in_=pair["o0"])
+
         def plain_half(c):
             nc.scalar.copy(out=o0[c][:, 0:64], in_=o1[c][:, 0:64])
 
@@ -376,12 +417,15 @@ def tile_deepseekv4attention_pa_kernel(tc, hidden_bytes, hidden_scale, wkv, wgat
                 if pc >= 1:
                     project(pc, 0)
                     evac_gate(pc, 0)
-                if sc >= 1:
-                    plain_half(sc - 1)
             if r == 1:
                 if sc >= 0:
                     expo(sc, 0)
                     weigh_lo(sc, nc.gpsimd)
+                if i == 5:
+                    project(0, 0)
+                    evac_gate(0, 0)
+                    project(0, 1)
+                    evac_gate(0, 1)
                 if pc >= 1:
                     project(pc, 1)
                     evac_gate(pc, 1)
@@ -389,17 +433,12 @@ def tile_deepseekv4attention_pa_kernel(tc, hidden_bytes, hidden_scale, wkv, wgat
                     expo(sc, 1)
             if r == 2:
                 if i == 6:
-                    project(0, 0)
-                    evac_gate(0, 0)
-                    project(0, 1)
-                    evac_gate(0, 1)
+                    project(0, 2)
+                    evac_kvlo(0)
                 if pc >= 1:
                     project(pc, 2)
                     evac_kvlo(pc)
             if r == 3:
-                if i == 7:
-                    project(0, 2)
-                    evac_kvlo(0)
                 if sc >= 0:
                     sum_z(sc)
             if LEAD <= i + LEAD < NT:
@@ -410,7 +449,7 @@ def tile_deepseekv4attention_pa_kernel(tc, hidden_bytes, hidden_scale, wkv, wgat
                 sin_tables()
             if i not in SPATH:
                 mult(i)
-            if i == 5:
+            if i == 4:
                 quantize_hidden(0, 0)
                 quantize_hidden(0, 1)
                 quantize_w(0)
@@ -419,7 +458,6 @@ def tile_deepseekv4attention_pa_kernel(tc, hidden_bytes, hidden_scale, wkv, wgat
                 if sc >= 0:
                     weigh_hi(sc)
                     sum_a(sc)
-                    recip(sc)
                 if pc >= 0:
                     max1(pc)
                     project(pc, 3)
@@ -431,20 +469,12 @@ def tile_deepseekv4attention_pa_kernel(tc, hidden_bytes, hidden_scale, wkv, wgat
                     spath_a(i + 1, 1)
                     turn(i + 2)
                     turned.add(i + 2)
-                if sc >= 1:
-                    rot_add(sc - 1)
-                    store0(sc - 1)
                 if c > 0:
                     quantize_hidden(c, 1)
                 if pc >= 0:
                     max2(pc)
-                if sc >= 0:
-                    norm(sc)
                 if c > 0:
                     quantize_hidden(c, 0)
-                if sc >= 0:
-                    rot_a(sc)
-                    rot_b(sc)
                 if pc >= 0:
                     max3(pc)
         weigh_hi(1)
@@ -463,17 +493,15 @@ def tile_deepseekv4attention_pa_kernel(tc, hidden_bytes, hidden_scale, wkv, wgat
         project(3, 2, (0, 1), ps_xt)
         project(3, 3, (0, 1), ps_xt)
         max1(2)
-        recip(1)
+        recip01()
         max_pair(3, 1)
         max2(2)
-        rot_add(0)
-        store0(0)
-        norm(1)
-        plain_half(1)
+        norm01()
+        plain01()
         max_pair(3, 0)
         max3(2)
-        rot_a(1)
-        rot_b(1)
+        rot_a01()
+        rot_b01()
         max_join(3)
         shift(2, 0, nc.vector)
         expo(2, 0)
@@ -493,8 +521,8 @@ def tile_deepseekv4attention_pa_kernel(tc, hidden_bytes, hidden_scale, wkv, wgat
         idle(2)
         weigh_hi(2)
         sum_a(2)
-        rot_add(1)
-        store0(1)
+        rot_add01()
+        store01()
         recip(2)
         weigh_lo(3, nc.vector)
         recip(3)

import math
from contextlib import ExitStack

import concourse.mybir as mybir
from concourse.masks import make_identity

FLOPS = 2 * 2048 * 1024 * 512

F32 = mybir.dt.float32
BF16 = mybir.dt.bfloat16
I32 = mybir.dt.int32
U32 = mybir.dt.uint32
U8 = mybir.dt.uint8
FP8 = mybir.dt.float8_e4m3fn
FP8X4 = mybir.dt.float8_e4m3fn_x4
ALU = mybir.AluOpType
ACT = mybir.ActivationFunctionType

P = 128
HID = 1024
NW = 512
RATIO = 4
NCH = 4
NT = RATIO * NCH
HALF = 32
THETA = 10000.0
GW = 520
TWO_PI = 2.0 * math.pi
SPATH = (12,)
LEAD = 4
VCAST = (1,)


def tile_deepseekv4attention_pa_kernel(tc, hidden_bytes, hidden_scale, wkv, wgate, ape, out_0, out_1):
    nc = tc.nc
    hb_view = hidden_bytes.rearrange("o (c w r) k -> o c r w k", c=NCH, w=P, r=RATIO)[0]
    o0_view = out_0.rearrange("o (c p) f -> o c p f", p=P)[0]
    o1_view = out_1.rearrange("o (c p) f -> o c p f", p=P)[0]

    with ExitStack() as ctx:
        const = ctx.enter_context(tc.tile_pool(name="const", bufs=1))
        bytes_pool = ctx.enter_context(tc.tile_pool(name="bytes", bufs=1))
        xb_pool = ctx.enter_context(tc.tile_pool(name="xb", bufs=6))
        grp_pool = ctx.enter_context(tc.tile_pool(name="grp", bufs=2))
        code_pool = ctx.enter_context(tc.tile_pool(name="codes", bufs=2))
        fin_pool = ctx.enter_context(tc.tile_pool(name="fin", bufs=2))
        ps_xt = ctx.enter_context(tc.psum_pool(name="ps_xt", bufs=3))
        ps_ab = ctx.enter_context(tc.psum_pool(name="ps_ab", bufs=2))
        ps_k = ctx.enter_context(tc.psum_pool(name="ps_k", bufs=1))
        ps_sum = ctx.enter_context(tc.psum_pool(name="ps_sum", bufs=1))
        ctx.enter_context(tc.manual_schedule())

        scale_col = const.tile([P, 2, 4], F32, name="scale_col")
        hb = {}

        def load_bytes(i):
            t = bytes_pool.tile([P, HID], U8, name="hb_%d" % i)
            nc.sync.dma_start(out=t, in_=hb_view[i // RATIO, i % RATIO])
            hb[i] = t

        wraw = {}

        def load_w(key, w):
            t = const.tile([P, 2, 4, 256], BF16, name="wraw_" + key)
            nc.sync.dma_start(out=t, in_=w.rearrange("(g p j) n -> p g j n", g=2, p=P, j=4))
            wraw[key] = t

        load_bytes(0)
        nc.sync.dma_start(out=scale_col, in_=hidden_scale.rearrange("a b (g p t) -> (a b p) g t", g=2, t=4))
        load_bytes(1)
        load_bytes(2)
        load_w("gate", wgate)
        load_bytes(3)
        load_bytes(4)
        load_w("kv", wkv)
        for i in range(5, 8):
            load_bytes(i)
        ape_b = []
        with nc.allow_non_contiguous_dma(reason="ape: 1024 values, one feature to a partition"):
            for h in range(2):
                t = const.tile([P, RATIO], BF16, name="ape_b%d" % h)
                nc.sync.dma_start(out=t, in_=ape[:, h * P:(h + 1) * P].rearrange("r f -> f r"))
                ape_b.append(t)
        for i in range(8, NT):
            load_bytes(i)

        pos = const.tile([P, NCH], F32, name="pos")
        nc.gpsimd.iota(pos, pattern=[[RATIO * P, NCH]], base=0, channel_multiplier=RATIO, allow_small_or_imprecise_dtypes=True)
        ident = const.tile([P, P], F32, name="ident")
        make_identity(nc, ident)
        first = const.tile([P, 2], F32, name="first")
        nc.scalar.activation(out=first, in_=ident[:, 0:2], func=ACT.Sin, scale=0.0)
        g8 = const.tile([P, 8, GW], F32, name="g8")
        kv4 = const.tile([P, 4, GW], F32, name="kv4")
        nc.gpsimd.memset(g8[:, 0:4, 0:1], -1.0e30)
        nc.gpsimd.memset(kv4[:, :, 0:1], 0.0)

        coarse = const.tile([P, NCH, 4], F32, name="coarse")
        turns = const.tile([P, NCH * 4, 8], F32, name="turns")
        turns_f = turns.rearrange("p q b -> p (q b)")
        whole_i = const.tile([P, NCH * HALF], I32, name="whole_i")
        whole = const.tile([P, NCH * HALF], F32, name="whole")
        frac = const.tile([P, NCH * HALF], F32, name="frac")
        frac_c = const.tile([P, NCH * HALF], F32, name="frac_c")
        neg_s = const.tile([P, NCH * HALF], F32, name="neg_s")
        neg_c = const.tile([P, NCH * HALF], F32, name="neg_c")
        for a in range(4):
            nc.vector.tensor_scalar(out=coarse[:, :, a], in0=pos, scalar1=THETA ** (-8 * a / HALF), scalar2=None, op0=ALU.mult)
        for b in range(8):
            nc.vector.tensor_scalar(out=turns[:, :, b], in0=coarse.rearrange("p c a -> p (c a)"), scalar1=THETA ** (-b / HALF) / TWO_PI, scalar2=None, op0=ALU.mult)
        nc.vector.tensor_copy(out=whole_i, in_=turns_f)

        def table_step(k):
            if k == 0:
                nc.vector.tensor_copy(out=whole, in_=whole_i)
            if k == 1:
                nc.vector.tensor_tensor(out=frac, in0=turns_f, in1=whole, op=ALU.subtract)
            if k == 2:
                nc.vector.tensor_scalar(out=frac_c, in0=frac, scalar1=0.25, scalar2=None, op0=ALU.add)
                nc.vector.scalar_tensor_tensor(out=neg_s, in0=frac, scalar=0.5, in1=frac, op0=ALU.is_gt, op1=ALU.subtract)
            if k == 3:
                nc.vector.scalar_tensor_tensor(out=neg_c, in0=frac_c, scalar=0.5, in1=frac_c, op0=ALU.is_gt, op1=ALU.subtract)

        cc = const.tile([P, NCH * HALF, 2], F32, name="cc")
        ss = const.tile([P, NCH * HALF, 2], F32, name="ss")

        def sin_tables():
            nc.scalar.activation(out=ss[:, :, 0], in_=neg_s, func=ACT.Sin, scale=TWO_PI)
            nc.scalar.activation(out=ss[:, :, 1], in_=neg_s, func=ACT.Sin, scale=-TWO_PI)
            nc.scalar.activation(out=cc[:, :, 0], in_=neg_c, func=ACT.Sin, scale=-TWO_PI)
            nc.scalar.activation(out=cc[:, :, 1], in_=neg_c, func=ACT.Sin, scale=-TWO_PI)
            warm = const.tile([P, 2], F32, name="warm")
            nc.scalar.activation(out=warm, in_=cc[:, 0, :], func=ACT.Exp, scale=0.0)

        wgrp = const.tile([P, 2, 2, 256, 4], BF16, name="wgrp", align_bytes=64)
        wcodes = const.tile([P, 1024], U32, name="wcodes", align_bytes=64)
        wscales = const.tile([P, 1024], U8, name="wscales", align_bytes=64)
        KEYS = ("gate", "kv")

        def interleave_w(kind, g):
            nc.gpsimd.tensor_scalar(out=wgrp[:, kind, g], in0=wraw[KEYS[kind]][:, g].rearrange("p j n -> p n j"), scalar1=1.0, scalar2=0.0, op0=ALU.mult, op1=ALU.add)

        def quantize_w(kind):
            cols = slice(512 * kind, 512 * (kind + 1))
            nc.vector.quantize_mx(out=wcodes[:, cols].bitcast(FP8X4), scales=wscales[:, cols], in_=wgrp[:, kind].rearrange("p g n j -> p (g n j)"))

        for kind in range(2):
            for g in range(2):
                interleave_w(kind, g)

        xb = {}
        planes = {}
        xt = {}
        grp = {}
        hcodes = {}
        hscales = {}
        acc = {}

        def cast(i):
            xb[i] = xb_pool.tile([P, HID], BF16, name="xb")
            if i == 0:
                nc.scalar.copy(out=xb[i][:, 0:512], in_=hb[i][:, 0:512].bitcast(FP8))
                nc.vector.tensor_copy(out=xb[i][:, 512:1024], in_=hb[i][:, 512:1024].bitcast(FP8))
            elif i in VCAST:
                nc.vector.tensor_copy(out=xb[i], in_=hb[i].bitcast(FP8))
            else:
                nc.scalar.copy(out=xb[i], in_=hb[i].bitcast(FP8))

        def turn(i):
            words = xb[i].bitcast(F32)
            xt[i] = ps_xt.tile([P, 2, P, 2], F32, name="xt")
            for g in range(2):
                for u in range(2):
                    nc.tensor.transpose(xt[i][:, g, :, u], words[:, 256 * g + u:256 * (g + 1):2], ident)

        def mult(i):
            c, r = divmod(i, RATIO)
            nc.vector.tensor_tensor(
                out=grp[c].rearrange("p (h g r x) -> p h g r x", h=2, g=2, r=2)[:, r // 2, :, r % 2, :].rearrange("p g (w t) -> p g w t", t=4),
                in0=xt[i].rearrange("p g w u -> p (g w u)").bitcast(BF16).rearrange("p (g w t) -> p g w t", g=2, t=4),
                in1=scale_col.unsqueeze(2).to_broadcast([P, 2, P, 4]),
                op=ALU.mult,
            )

        def spath_a(i, g):
            if g == 0:
                planes[i] = fin_pool.tile([P, 2, 4, P], BF16, name="planes")
            xv = xt[i].rearrange("p g w u -> p (g w u)").bitcast(BF16).rearrange("p (g w t) -> p g t w", g=2, t=4)
            for t in range(4):
                nc.scalar.activation(out=planes[i][:, g, t, :], in_=xv[:, g, t, :], func=ACT.Copy, scale=scale_col[:, g, t:t + 1])

        def spath_b(i):
            c, r = divmod(i, RATIO)
            nc.scalar.copy(
                out=grp[c].rearrange("p (h g r x) -> p h g r x", h=2, g=2, r=2)[:, r // 2, :, r % 2, :].rearrange("p g (w t) -> p g w t", t=4),
                in_=planes[i].rearrange("p g t w -> p g w t"),
            )

        def quantize_hidden(c, h):
            if c not in hcodes:
                hcodes[c] = code_pool.tile([P, 1024], U32, name="hcodes", align_bytes=64)
                hscales[c] = code_pool.tile([P, 1024], U8, name="hscales", align_bytes=64)
            cols = slice(512 * h, 512 * (h + 1))
            nc.vector.quantize_mx(out=hcodes[c][:, cols].bitcast(FP8X4), scales=hscales[c][:, cols], in_=grp[c][:, 2048 * h:2048 * (h + 1)])

        def project(c, m, halves=(0, 1), pool=None):
            kind, hi = divmod(m, 2)
            if (c, m) not in acc:
                if pool is not None:
                    acc[c, m] = pool.tile([P, NW], F32, name="xt")
                elif m == 3:
                    acc[c, m] = ps_k.tile([P, NW], F32, name="kvhi")
                else:
                    acc[c, m] = ps_ab.tile([P, NW], F32, name="ab")
            for h in halves:
                for g in range(2):
                    wc = slice(512 * kind + 256 * g + P * hi, 512 * kind + 256 * g + P * (hi + 1))
                    hc = slice(512 * h + 256 * g, 512 * h + 256 * (g + 1))
                    nc.tensor.matmul_mx(
                        out=acc[c, m][:, 256 * h:256 * (h + 1)],
                        lhsT=wcodes[:, wc].bitcast(FP8X4), lhsT_scale=wscales[:, wc],
                        rhs=hcodes[c][:, hc].bitcast(FP8X4), rhs_scale=hscales[c][:, hc],
                        start=(g == 0), stop=(g == 1),
                    )

        def evac_gate(c, hi, slots=(0, 1, 2, 3)):
            for r in slots:
                s = 4 * hi + r
                cols = slice(1 - hi + c * P, 1 - hi + (c + 1) * P)
                nc.scalar.activation(out=g8[:, s, cols], in_=acc[c, hi][:, r * P:(r + 1) * P], func=ACT.Identity, bias=ape_b[hi][:, r:r + 1], scale=1.0)

        def evac_kvlo(c):
            nc.scalar.copy(out=kv4[:, :, 1 + c * P:1 + (c + 1) * P], in_=acc[c, 2].rearrange("p (r w) -> p r w", r=RATIO))

        m4 = {}
        m2 = {}
        gm = {}
        e8 = {}
        p8 = {}
        zt = {}
        at = {}
        rz = {}
        o1 = {}
        o0 = {}
        t1 = {}
        t2 = {}
        crz = {}
        srz = {}

        def max1(c):
            cols = slice(c * P, (c + 1) * P)
            m4[c] = fin_pool.tile([P, 4, P], F32, name="m4")
            nc.vector.tensor_tensor(out=m4[c], in0=g8[:, 0:4, cols], in1=g8[:, 4:8, cols], op=ALU.max)

        def max2(c):
            m2[c] = fin_pool.tile([P, 2, P], F32, name="m2")
            nc.vector.tensor_tensor(out=m2[c], in0=m4[c][:, 0:2, :], in1=m4[c][:, 2:4, :], op=ALU.max)

        def max3(c):
            gm[c] = fin_pool.tile([P, P], F32, name="gm")
            nc.vector.tensor_tensor(out=gm[c], in0=m2[c][:, 0, :], in1=m2[c][:, 1, :], op=ALU.max)

        def max_pair(c, h):
            cols = slice(c * P, (c + 1) * P)
            m4[c, h] = fin_pool.tile([P, 2, P], F32, name="mp%d" % h)
            nc.vector.tensor_tensor(out=m4[c, h], in0=g8[:, 2 * h:2 * h + 2, cols], in1=g8[:, 4 + 2 * h:6 + 2 * h, cols], op=ALU.max)

        def max_join(c):
            m2[c] = fin_pool.tile([P, 2, P], F32, name="m2")
            nc.vector.tensor_tensor(out=m2[c], in0=m4[c, 0], in1=m4[c, 1], op=ALU.max)

        def shift(c, hi, eng):
            cols = slice(c * P, (c + 1) * P)
            if hi == 0:
                e8[c] = fin_pool.tile([P, 8, P], F32, name="e8")
            rows = slice(4 * hi, 4 * hi + 4)
            eng.tensor_tensor(out=e8[c][:, rows, :], in0=g8[:, rows, cols], in1=gm[c].unsqueeze(1).to_broadcast([P, 4, P]), op=ALU.subtract)

        def expo(c, hi):
            rows = slice(4 * hi, 4 * hi + 4)
            nc.scalar.activation(out=e8[c][:, rows, :], in_=e8[c][:, rows, :], func=ACT.Exp)

        pair = {}

        def sum_z(c):
            if c == 0:
                pair["z"] = ps_sum.tile([P, 2, P], F32, name="zt")
            if c < 2:
                zt[c] = pair["z"][:, c, :]
            else:
                zt[c] = ps_sum.tile([P, P], F32, name="zt") if c < 3 else ps_xt.tile([P, P], F32, name="xt")
            for s in range(8):
                nc.tensor.matmul(out=zt[c], lhsT=e8[c][:, s, :], rhs=ident, is_transpose=True, start=(s == 0), stop=(s == 7))

        def weigh_lo(c, eng):
            cols = slice(c * P, (c + 1) * P)
            p8[c] = fin_pool.tile([P, 8, P], F32, name="p8")
            eng.tensor_tensor(out=p8[c][:, 0:4, :], in0=e8[c][:, 0:4, :], in1=kv4[:, :, cols], op=ALU.mult)

        def weigh_hi(c):
            nc.vector.tensor_tensor(out=p8[c][:, 4:8, :], in0=e8[c][:, 4:8, :], in1=acc[c, 3].rearrange("p (r w) -> p r w", r=RATIO), op=ALU.mult)

        def sum_a(c):
            if c == 0:
                pair["a"] = ps_sum.tile([P, 2, P], F32, name="at")
            if c < 2:
                at[c] = pair["a"][:, c, :]
            else:
                at[c] = ps_sum.tile([P, P], F32, name="at") if c < 3 else ps_ab.tile([P, P], F32, name="ab")
            for s in range(8):
                nc.tensor.matmul(out=at[c], lhsT=p8[c][:, s, :], rhs=ident, is_transpose=True, start=(s == 0), stop=(s == 7))

        def recip(c):
            rz[c] = fin_pool.tile([P, P], F32, name="rz")
            nc.vector.reciprocal(out=rz[c], in_=zt[c])

        def norm(c):
            o1[c] = fin_pool.tile([P, P], F32, name="o1")
            nc.vector.tensor_tensor(out=o1[c], in0=at[c], in1=rz[c], op=ALU.mult)
            nc.sync.dma_start(out=o1_view[c], in_=o1[c])
            o0[c] = fin_pool.tile([P, P], F32, name="o0")

        def rot_a(c):
            rot = o1[c][:, 64:128].rearrange("p (j e) -> p j e", e=2)
            t1[c] = fin_pool.tile([P, HALF, 2], F32, name="t1")
            nc.vector.tensor_tensor(out=t1[c], in0=rot, in1=cc[:, c * HALF:(c + 1) * HALF, :], op=ALU.mult)

        def rot_b(c):
            rot = o1[c][:, 64:128].rearrange("p (j e) -> p j e", e=2)
            t2[c] = fin_pool.tile([P, HALF, 2], F32, name="t2")
            nc.vector.tensor_tensor(out=t2[c], in0=rot[:, :, ::-1], in1=ss[:, c * HALF:(c + 1) * HALF, :], op=ALU.mult)

        def rot_add(c):
            nc.vector.tensor_tensor(out=o0[c][:, 64:128].rearrange("p (j e) -> p j e", e=2), in0=t1[c], in1=t2[c], op=ALU.add)

        def fold_tables(c):
            rzr = rz[c][:, 64:128].rearrange("p (j e) -> p j e", e=2)
            tj = slice(c * HALF, (c + 1) * HALF)
            crz[c] = fin_pool.tile([P, HALF, 2], F32, name="crz")
            srz[c] = fin_pool.tile([P, HALF, 2], F32, name="srz")
            nc.vector.tensor_tensor(out=crz[c], in0=rzr, in1=cc[:, tj, :], op=ALU.mult)
            nc.vector.tensor_tensor(out=srz[c], in0=rzr[:, :, ::-1], in1=ss[:, tj, :], op=ALU.mult)

        def rot_folded(c):
            atr = at[c][:, 64:128].rearrange("p (j e) -> p j e", e=2)
            t1[c] = fin_pool.tile([P, HALF, 2], F32, name="t1")
            t2[c] = fin_pool.tile([P, HALF, 2], F32, name="t2")
            nc.vector.tensor_tensor(out=t1[c], in0=atr, in1=crz[c], op=ALU.mult)
            nc.vector.tensor_tensor(out=t2[c], in0=atr[:, :, ::-1], in1=srz[c], op=ALU.mult)

        def recip01():
            pair["rz"] = fin_pool.tile([P, 2, P], F32, name="rz01")
            nc.vector.reciprocal(out=pair["rz"], in_=pair["z"])

        def norm01():
            pair["o1"] = fin_pool.tile([P, 2, P], F32, name="o1p")
            nc.vector.tensor_tensor(out=pair["o1"], in0=pair["a"], in1=pair["rz"], op=ALU.mult)
            nc.sync.dma_start(out=o1_view[0:2].rearrange("c p f -> p c f"), in_=pair["o1"])
            pair["o0"] = fin_pool.tile([P, 2, P], F32, name="o0p")

        def rot_a01():
            rot = pair["o1"][:, :, 64:128].rearrange("p c (j e) -> p c j e", e=2)
            pair["t1"] = fin_pool.tile([P, 2, HALF, 2], F32, name="t1p")
            nc.vector.tensor_tensor(out=pair["t1"], in0=rot, in1=cc[:, 0:2 * HALF, :].rearrange("p (c j) e -> p c j e", c=2), op=ALU.mult)

        def rot_b01():
            rot = pair["o1"][:, :, 64:128].rearrange("p c (j e) -> p c j e", e=2)
            pair["t2"] = fin_pool.tile([P, 2, HALF, 2], F32, name="t2p")
            nc.vector.tensor_tensor(out=pair["t2"], in0=rot[:, :, :, ::-1], in1=ss[:, 0:2 * HALF, :].rearrange("p (c j) e -> p c j e", c=2), op=ALU.mult)

        def rot_add01():
            nc.vector.tensor_tensor(out=pair["o0"][:, :, 64:128].rearrange("p c (j e) -> p c j e", e=2), in0=pair["t1"], in1=pair["t2"], op=ALU.add)

        def plain01():
            nc.scalar.copy(out=pair["o0"][:, :, 0:64], in_=pair["o1"][:, :, 0:64])

        def store01():
            nc.sync.dma_start(out=o0_view[0:2].rearrange("c p f -> p c f"), in_=pair["o0"])

        def plain_half(c):
            nc.scalar.copy(out=o0[c][:, 0:64], in_=o1[c][:, 0:64])

        def store0(c):
            nc.sync.dma_start(out=o0_view[c], in_=o0[c])

        idle_ps = {}

        def idle(n):
            for k in range(n):
                nc.tensor.matmul(out=idle_ps[0], lhsT=ident, rhs=ident, start=True, stop=True)

        idle_ps[0] = ps_sum.tile([P, P], F32, name="zt")
        idle(4)
        table_step(0)
        table_step(1)
        cast(0)
        table_step(2)
        cast(1)
        cast(2)
        cast(3)
        table_step(3)
        turn(0)
        turned = {0}
        for i in range(NT):
            c, r = divmod(i, RATIO)
            pc = c - 1
            sc = c - 2
            if r == 0:
                grp[c] = grp_pool.tile([P, 4 * HID], BF16, name="grp", align_bytes=64)
            if i + 1 < NT and (r != 3 or c == 0) and i + 1 not in turned:
                turn(i + 1)
                turned.add(i + 1)
            if r == 0:
                if sc >= 0:
                    shift(sc, 0, nc.gpsimd)
                    shift(sc, 1, nc.gpsimd)
                if pc >= 1:
                    project(pc, 0)
                    evac_gate(pc, 0)
            if r == 1:
                if sc >= 0:
                    expo(sc, 0)
                    weigh_lo(sc, nc.gpsimd)
                if i == 5:
                    project(0, 0)
                    evac_gate(0, 0)
                    project(0, 1)
                    evac_gate(0, 1)
                if pc >= 1:
                    project(pc, 1)
                    evac_gate(pc, 1)
                if sc >= 0:
                    expo(sc, 1)
            if r == 2:
                if i == 6:
                    project(0, 2)
                    evac_kvlo(0)
                if pc >= 1:
                    project(pc, 2)
                    evac_kvlo(pc)
            if r == 3:
                if sc >= 0:
                    sum_z(sc)
            if LEAD <= i + LEAD < NT:
                cast(i + LEAD)
            if i - 1 in SPATH:
                spath_b(i - 1)
            if i == 3:
                sin_tables()
            if i not in SPATH:
                mult(i)
            if i == 4:
                quantize_hidden(0, 0)
                quantize_hidden(0, 1)
                quantize_w(0)
                quantize_w(1)
            if r == 3 and c < 3:
                if sc >= 0:
                    weigh_hi(sc)
                    sum_a(sc)
                if pc >= 0:
                    max1(pc)
                    project(pc, 3)
                if i + 1 not in turned:
                    turn(i + 1)
                    turned.add(i + 1)
                if i + 1 in SPATH:
                    spath_a(i + 1, 0)
                    spath_a(i + 1, 1)
                    turn(i + 2)
                    turned.add(i + 2)
                if c > 0:
                    quantize_hidden(c, 1)
                if pc >= 0:
                    max2(pc)
                if c > 0:
                    quantize_hidden(c, 0)
                if pc >= 0:
                    max3(pc)
        weigh_hi(1)
        sum_a(1)
        project(2, 3)
        quantize_hidden(3, 1)
        project(3, 0, (1,))
        project(3, 1, (1,))
        evac_gate(3, 0, (2, 3))
        evac_gate(3, 1, (2, 3))
        quantize_hidden(3, 0)
        project(3, 0, (0,))
        project(3, 1, (0,))
        evac_gate(3, 0, (0, 1))
        evac_gate(3, 1, (0, 1))
        project(3, 2, (0, 1), ps_xt)
        project(3, 3, (0, 1), ps_xt)
        max1(2)
        recip01()
        max_pair(3, 1)
        max2(2)
        norm01()
        plain01()
        max_pair(3, 0)
        max3(2)
        rot_a01()
        rot_b01()
        max_join(3)
        shift(2, 0, nc.vector)
        expo(2, 0)
        max3(3)
        shift(2, 1, nc.vector)
        expo(2, 1)
        evac_kvlo(3)
        sum_z(2)
        idle_ps[0] = ps_ab.tile([P, P], F32, name="ab")
        idle(3)
        shift(3, 0, nc.vector)
        expo(3, 0)
        weigh_lo(2, nc.vector)
        shift(3, 1, nc.vector)
        expo(3, 1)
        sum_z(3)
        idle(2)
        weigh_hi(2)
        sum_a(2)
        rot_add01()
        store01()
        recip(2)
        weigh_lo(3, nc.vector)
        recip(3)
        weigh_hi(3)
        sum_a(3)
        norm(2)
        plain_half(2)
        fold_tables(3)
        rot_a(2)
        rot_b(2)
        rot_folded(3)
        norm(3)
        plain_half(3)
        rot_add(2)
        store0(2)
        rot_add(3)
        store0(3)
